import numpy as np
import ml_dtypes


def mxq(x, axis, fmt="e4m3"):
    dtype, down = {"e4m3": (ml_dtypes.float8_e4m3fn, 7), "e5m2": (ml_dtypes.float8_e5m2, 14)}[fmt]
    v = np.moveaxis(np.asarray(x, np.float32).astype(ml_dtypes.bfloat16).astype(np.float64), axis, -1)
    blocks = v.reshape(v.shape[:-1] + (-1, 32))
    amax = np.abs(blocks).max(-1, keepdims=True)
    byte = np.maximum(np.where(amax > 0, np.frexp(amax)[1] - 1 + 127, 0) - down, 1)
    scale = np.exp2(byte - 127.0)
    codes = (blocks / scale).astype(np.float32).astype(dtype).astype(np.float64)
    return np.moveaxis((codes * scale).reshape(v.shape), -1, axis)


WIDE = False


def mx_kscale(k):
    if not WIDE:
        return np.ones(k)
    levels = np.array([10, -10, 5, -5, 0])
    if k % 512:
        return np.exp2(np.random.permutation(np.resize(levels, k // 32))).repeat(32)
    a = np.empty((k // 512, 16))
    for p in range(k // 512):
        a[p, :8] = np.random.permutation(np.resize(levels, 8))
        for g in range(8):
            far = levels[np.abs(levels - a[p, g]) >= 10]
            a[p, g + 8] = far[np.random.randint(len(far))]
    return np.exp2(a.ravel()).repeat(32)


BF16 = ml_dtypes.bfloat16


def bf(x):
    return np.asarray(x, np.float32).astype(BF16)


def f64(x):
    return np.asarray(x).astype(np.float64)


E2M1 = np.array([0.0, 0.5, 1.0, 1.5, 2.0, 3.0, 4.0, 6.0, -0.0, -0.5, -1.0, -1.5, -2.0, -3.0, -4.0, -6.0])


def pack_weight(w, fmt):
    k, n = w.shape
    w = f64(bf(w)).reshape(k // 32, 32, n)
    amax = np.abs(w).max(1)
    if fmt == "e4m3":
        byte = np.frexp(amax)[1] - 1 + 127 - 7
    else:
        mant, ex = np.frexp(amax / 6.0)
        byte = np.where(mant > 0.5, ex, ex - 1) + 127
    byte = np.clip(np.where(amax > 0, byte, 1), 1, 254)
    scaled = (w * np.exp2(127.0 - byte)[:, None, :]).reshape(k, n).astype(np.float32)
    by_word = np.ascontiguousarray(scaled.reshape(k // 512, 128, 4, n).transpose(0, 1, 3, 2))
    if fmt == "e4m3":
        words = by_word.astype(ml_dtypes.float8_e4m3fn).view(np.uint8)
    else:
        c = by_word.astype(ml_dtypes.float4_e2m1fn).view(np.uint8) & 0xF
        words = c[..., 0::2] | (c[..., 1::2] << 4)
    return np.ascontiguousarray(words), np.ascontiguousarray(byte.astype(np.uint8).reshape(k // 512, 16, n))


def unpack_weight(words, scales, fmt):
    g, p, n, _ = words.shape
    if fmt == "e4m3":
        vals = np.ascontiguousarray(words).view(ml_dtypes.float8_e4m3fn).astype(np.float64)
    else:
        nib = np.empty((g, p, n, 4), np.uint8)
        nib[..., 0::2] = words & 0xF
        nib[..., 1::2] = words >> 4
        vals = E2M1[nib]
    vals = vals * np.repeat(np.exp2(scales.astype(np.float64) - 127.0), 8, axis=1)[..., None]
    return vals.transpose(0, 1, 3, 2).reshape(g * 512, n)


B, D, S, O = 1024, 512, 1024, 256
K1 = D + S
P = S // 2
EPS = 1e-6


def sigmoid(v):
    return 1.0 / (1.0 + np.exp(-v))


def draw0():
    r = np.random.standard_normal
    s = np.concatenate([mx_kscale(D), np.ones(S)])
    t = mx_kscale(S)
    inputs = bf(r((B, D)) * s[:D])
    states = bf(r((B, S)))
    W1_words, W1_scales = pack_weight(r((K1, S)) / np.sqrt(K1) / s[:, None] * t, "e4m3")
    b1 = bf(r(S) * 0.2 * t)
    W2_words, W2_scales = pack_weight(r((S, P)) / np.sqrt(S) / t[:, None], "e4m3")
    return {
        "inputs": inputs,
        "states": states,
        "W1_words": W1_words,
        "W1_scales": W1_scales,
        "b1": b1,
        "W2_words": W2_words,
        "W2_scales": W2_scales,
        "b2": bf(r(P) * 0.2),
        "excitatory_potential": bf(1.0 + 0.1 * r(S)),
        "inhibitory_potential": bf(-1.0 + 0.1 * r(S)),
        "capacitance": bf(1.0 + 0.1 * r(S)),
        "max_conductance": bf(1.0 + 0.1 * r((S, 2))),
        "mean_conductance_potential": bf(0.3 * r((S, 2))),
        "std_conductance": bf(1.0 + 0.2 * r((S, 2))),
        "gamma": bf(1.0 + 0.1 * r(S)),
        "beta": bf(0.1 * r(S)),
    }


def core(inputs, states, W1_words, W1_scales, b1, W2_words, W2_scales, b2, excitatory_potential, inhibitory_potential, capacitance,
              max_conductance, mean_conductance_potential, std_conductance, gamma, beta):
    v = f64(states)
    b, s = v.shape
    intervals = np.ones((b, 1))
    cat = np.concatenate([f64(inputs), v], -1)
    h = (mxq(cat, 1, "e4m3") @ unpack_weight(W1_words, W1_scales, "e4m3")) + f64(b1)
    pre = (mxq(h, 1, "e4m3") @ unpack_weight(W2_words, W2_scales, "e4m3")) + f64(b2)
    memory_cell_inputs = np.stack([pre, -pre], -1).reshape(b, s)
    pairs = v.reshape(b, s // 2, 2)
    rolled = np.roll(pairs, 1, axis=-1)
    presyn = np.concatenate([pairs, rolled], -1).reshape(b, s, 2)
    g = f64(max_conductance) * sigmoid(f64(std_conductance) * (presyn - f64(mean_conductance_potential)))
    rev = np.stack([f64(excitatory_potential), f64(inhibitory_potential)], -1)
    diff = rev - v[..., None]
    states_change = (memory_cell_inputs + np.sum(g * diff, -1)) / f64(capacitance) * intervals
    x = v + states_change
    mu = np.mean(x, -1, keepdims=True)
    var = np.mean((x - mu) ** 2, -1, keepdims=True)
    return (x - mu) * (1.0 / np.sqrt(var + EPS)) * f64(gamma) + f64(beta)


def e4m3fn_bytes(y):
    return np.clip(np.asarray(y, np.float64), -448.0, 448.0).astype(np.float32).astype(ml_dtypes.float8_e4m3fn).view(np.uint8)


def e4m3fn_values(b):
    return np.asarray(b, np.uint8).view(ml_dtypes.float8_e4m3fn).astype(np.float64)


def setup_inputs():
    d = draw0()
    x0 = np.asarray(d['inputs']).astype(np.float64)
    s = (np.max(np.abs(x0), axis=(0,), keepdims=True) / 448.0).astype(np.float32)
    out = {}
    for k, v in d.items():
        if k == 'inputs':
            out['inputs_bytes'] = e4m3fn_bytes(x0 / s.astype(np.float64))
            out['inputs_scale'] = s
        else:
            out[k] = v
    return out


def reference(inputs_bytes, inputs_scale, states, W1_words, W1_scales, b1, W2_words, W2_scales, b2, excitatory_potential, inhibitory_potential, capacitance, max_conductance, mean_conductance_potential, std_conductance, gamma, beta):
    return core(e4m3fn_values(inputs_bytes) * inputs_scale.astype(np.float64), states, W1_words, W1_scales, b1, W2_words, W2_scales, b2, excitatory_potential, inhibitory_potential, capacitance, max_conductance, mean_conductance_potential, std_conductance, gamma, beta)

@@ -1,0 +1,434 @@
+from contextlib import ExitStack
+
+import concourse.mybir as mybir
+from concourse.masks import make_identity
+
+F32 = mybir.dt.float32
+BF16 = mybir.dt.bfloat16
+I32 = mybir.dt.int32
+U8 = mybir.dt.uint8
+FP8 = mybir.dt.float8_e4m3fn
+FP8X4 = mybir.dt.float8_e4m3fn_x4
+ALU = mybir.AluOpType
+ACT = mybir.ActivationFunctionType
+
+FLOPS = 2 * 1024 * (1536 * 1024 + 1024 * 512)
+
+
+def tile_memorylayercell_pa_w8_kernel(
+    tc, inputs_bytes, inputs_scale, states, W1_words, W1_scales, b1, W2_words, W2_scales, b2,
+    excitatory_potential, inhibitory_potential, capacitance, max_conductance,
+    mean_conductance_potential, std_conductance, gamma, beta, out):
+    nc = tc.nc
+    with ExitStack() as ctx:
+        keep = ctx.enter_context(tc.tile_pool(name="keep", bufs=1))
+        work = ctx.enter_context(tc.tile_pool(name="work", bufs=2))
+        psum = ctx.enter_context(tc.psum_pool(name="psum", bufs=2))
+
+        pr2 = keep.tile([128, 1024], BF16, name="pr2")
+        pr1 = keep.tile([128, 512], BF16, name="pr1")
+        prb = keep.tile([128, 1024], BF16, name="prb")
+        prf = keep.tile([128, 512], F32, name="prf")
+        sts = [keep.tile([128, 2, 1024], BF16, name="sts%d" % k) for k in range(4)]
+        xb = [keep.tile([128, 2, 512], U8, name="xb%d" % k) for k in range(4)]
+        scl = keep.tile([128, 512], F32, name="scl")
+        w1w = [keep.tile([128, 1024], I32, name="w1w%d" % k, align_bytes=64) for k in range(3)]
+        w1s = keep.tile([128, 1024], U8, name="w1s", align_bytes=64)
+        w2w = keep.tile([128, 2, 512], I32, name="w2w", align_bytes=64)
+        w2p = keep.tile([128, 2, 512], I32, name="w2p", align_bytes=64)
+        w2s = keep.tile([128, 512], U8, name="w2s", align_bytes=64)
+        w2sp = keep.tile([128, 512], U8, name="w2sp", align_bytes=64)
+        b1c = keep.tile([128, 1024], BF16, name="b1c")
+        gmc = keep.tile([128, 1024], BF16, name="gmc")
+        btc = keep.tile([128, 1024], BF16, name="btc")
+        ident = keep.tile([128, 128], F32, name="ident")
+        mhalf = keep.tile([128, 1], F32, name="mhalf")
+        warm = keep.tile([128, 1], F32, name="warm")
+
+        def load_states(k):
+            nc.sync.dma_start(out=sts[k][:], in_=states[256 * k : 256 * k + 256, :].rearrange("(i p) s -> p i s", p=128))
+
+        def load_bytes(k):
+            nc.sync.dma_start(out=xb[k][:], in_=inputs_bytes[256 * k : 256 * k + 256, :].rearrange("(i p) k -> p i k", p=128))
+
+        def load_rows2(n, src):
+            nc.scalar.dma_start(out=pr2[2 * n : 2 * n + 2, :], in_=src.rearrange("(g x) c -> g (x c)", g=2))
+
+        def load_rows1(n, src):
+            nc.scalar.dma_start(out=pr1[2 * n : 2 * n + 2, :], in_=src.rearrange("(g x) -> g x", g=2))
+
+        def load_w1(k):
+            nc.sync.dma_start(out=w1w[k][:], in_=W1_words[k].rearrange("p n t -> p (n t)").bitcast(I32))
+
+        nc.vector.memset(pr2[:].bitcast(I32), 0)
+        nc.vector.memset(pr1[:].bitcast(I32), 0)
+        nc.vector.memset(prf[:], 0.0)
+        make_identity(nc, ident[:])
+        nc.gpsimd.memset(mhalf[:], -0.5)
+        nc.gpsimd.memset(prb[:].bitcast(I32), 0)
+        nc.gpsimd.memset(w1s[:].bitcast(I32), 0)
+        nc.gpsimd.memset(w2s[:].bitcast(I32), 0)
+        for j in range(2):
+            nc.sync.dma_start(out=sts[0][:, j, :], in_=states[128 * j : 128 * j + 128, :])
+        load_rows2(0, std_conductance)
+        load_rows2(1, mean_conductance_potential)
+        load_rows1(0, capacitance)
+        load_rows2(2, max_conductance)
+        nc.sync.dma_start(out=prf[0:1, :], in_=inputs_scale)
+        load_bytes(0)
+        load_rows1(1, excitatory_potential)
+        load_rows1(2, inhibitory_potential)
+        load_w1(1)
+        nc.scalar.dma_start(out=prb[0:1, :], in_=b1.unsqueeze(0))
+        nc.scalar.dma_start(out=pr1[6:8, 0:256], in_=b2.rearrange("(g x) -> g x", g=2))
+        load_w1(2)
+        load_w1(0)
+        for q in range(4):
+            nc.sync.dma_start(out=w1s[32 * q : 32 * q + 12, :].bitcast(I32), in_=W1_scales[:, 4 * q : 4 * q + 4, :].bitcast(I32))
+        load_states(1)
+        load_bytes(1)
+        nc.sync.dma_start(out=w2w[:].rearrange("p k n -> p k n"), in_=W2_words.rearrange("k p n t -> p k (n t)").bitcast(I32))
+        for q in range(4):
+            nc.sync.dma_start(out=w2s[32 * q : 32 * q + 8, :].bitcast(I32), in_=W2_scales[:, 4 * q : 4 * q + 4, :].bitcast(I32))
+        for k in range(2, 4):
+            load_states(k)
+            load_bytes(k)
+        nc.sync.dma_start(out=gmc[:], in_=gamma.partition_broadcast(128))
+        nc.sync.dma_start(out=btc[:], in_=beta.partition_broadcast(128))
+        nc.scalar.activation(out=warm[:], in_=mhalf[:], func=ACT.Sigmoid)
+
+        p2 = keep.tile([128, 6, 4, 2], BF16, name="p2")
+        p1 = keep.tile([128, 6, 2, 2], BF16, name="p1")
+        pb = keep.tile([128, 2, 2], BF16, name="pb")
+        sel = keep.tile([128, 1], BF16, name="sel")
+        stdf = keep.tile([128, 16], F32, name="stdf")
+        sbias = keep.tile([128, 16], F32, name="sbias")
+        icap = keep.tile([128, 8], F32, name="icap")
+        nab = keep.tile([128, 8, 2], F32, name="nab")
+        icpm = keep.tile([128, 4, 2], F32, name="icpm")
+        pbias = keep.tile([128, 4, 2], F32, name="pbias")
+
+        def flat2(n):
+            return p2[:, 2 * n : 2 * n + 2, :, :].rearrange("p g t c -> p (g t c)")
+
+        def flat1(n):
+            return p1[:, 2 * n : 2 * n + 2, :, :].rearrange("p g u e -> p (g u e)")
+
+        def sigmoid_parameters():
+            bank = psum.tile([128, 4, 128], F32, name="wT")
+            for t in range(4):
+                nc.tensor.transpose(bank[:, t, :], pr2[:].bitcast(F32)[:, t::4], ident[:])
+            nc.vector.tensor_copy(out=p2[:].rearrange("p r t c -> p r (t c)").bitcast(F32), in_=bank[:, :, 0:6].rearrange("p t r -> p r t"))
+            nc.vector.tensor_copy(out=stdf[:], in_=flat2(0))
+            nc.vector.scalar_tensor_tensor(out=sbias[:], in0=flat2(1), scalar=-1.0, in1=flat2(0), op0=ALU.mult, op1=ALU.mult)
+
+        def current_parameters():
+            bank = psum.tile([128, 4, 128], F32, name="wT")
+            for u in range(2):
+                nc.tensor.transpose(bank[:, u, :], pr1[:].bitcast(F32)[:, u::2], ident[:])
+            nc.tensor.transpose(bank[:, 2, :], pr1[:].bitcast(F32)[:, 0:128], ident[:])
+            nc.vector.tensor_copy(out=p1[:].rearrange("p r u e -> p r (u e)").bitcast(F32), in_=bank[:, 0:2, 0:6].rearrange("p u r -> p r u"))
+            nc.vector.tensor_copy(out=pb[:].rearrange("p g u -> p (g u)").bitcast(F32), in_=bank[:, 2, 6:8])
+            nc.vector.reciprocal(out=icap[:], in_=flat1(0))
+            nc.vector.scalar_tensor_tensor(
+                out=nab[:], in0=p2[:, 4:6, :, :].rearrange("p g t c -> p (g t) c"), scalar=-1.0,
+                in1=icap[:].unsqueeze(2).to_broadcast([128, 8, 2]), op0=ALU.mult, op1=ALU.mult)
+
+        def spread_scale():
+            bank = psum.tile([128, 512], F32, name="hp")
+            nc.tensor.matmul(bank[:], lhsT=ident[:, 0:1].to_broadcast([128, 128]), rhs=prf[:], start=True, stop=True)
+            nc.vector.tensor_copy(out=scl[:], in_=bank[:])
+
+        def spread_b1():
+            nc.vector.tensor_copy(out=sel[:], in_=ident[:, 0:1])
+            for n in range(2):
+                bank = psum.tile([128, 512], F32, name="hp")
+                nc.tensor.matmul(bank[:], lhsT=sel[:].to_broadcast([128, 128]), rhs=prb[:, 512 * n : 512 * n + 512], start=True, stop=True)
+                nc.vector.tensor_copy(out=b1c[:, 512 * n : 512 * n + 512], in_=bank[:])
+
+        def pre_parameters():
+            icv = icap[:].rearrange("p (q e) -> p q e", e=2)
+            nc.vector.tensor_copy(out=icpm[:, :, 0:1], in_=icv[:, :, 0:1])
+            nc.vector.tensor_scalar(out=icpm[:, :, 1:2], in0=icv[:, :, 1:2], scalar1=-1.0, scalar2=None, op0=ALU.mult)
+            nc.vector.tensor_tensor(
+                out=pbias[:], in0=icpm[:], in1=pb[:].rearrange("p g u -> p (g u)").unsqueeze(2).to_broadcast([128, 4, 2]), op=ALU.mult)
+            nc.vector.tensor_tensor(out=pbias[:], in0=pbias[:], in1=p1[:, 2:4, :, :].rearrange("p g u e -> p (g u) e"), op=ALU.add)
+
+        def exc(idx):
+            return p1[:, 2:4, :, :].rearrange("p g u e -> p (g u e)")[:, idx : idx + 1]
+
+        def inh(idx):
+            return p1[:, 4:6, :, :].rearrange("p g u e -> p (g u e)")[:, idx : idx + 1]
+
+        def permute_w2(k):
+            nc.vector.tensor_copy(out=w2p[:, k, :].rearrange("p (g u m) -> p g m u", g=2, u=2), in_=w2w[:, k, :].rearrange("p (g m u) -> p g m u", g=2, u=2))
+
+        def permute_w2_scales():
+            nc.vector.tensor_copy(out=w2sp[:].rearrange("p (g u m) -> p g m u", g=2, u=2), in_=w2s[:].rearrange("p (g m u) -> p g m u", g=2, u=2))
+
+        vT = {}
+        P0 = {}
+        P1 = {}
+        st = {}
+
+        def cat_words(k, kg):
+            bank = psum.tile([128, 2, 256], F32, name="wT")
+            for j in range(2):
+                src = st[k, "x", j][:] if kg == 0 else sts[k][:, j, :]
+                off = 0 if kg == 0 else 256 * (kg - 1)
+                for u in range(2):
+                    nc.tensor.transpose(bank[:, u, 128 * j : 128 * j + 128], src.bitcast(F32)[:, off + u : off + 256 : 2], ident[:])
+            st[k, "bank", kg] = bank
+
+        def cat_copy(k, kg, on_vector=False):
+            if kg == 0:
+                st[k, "q", 0] = work.tile([128, 256, 4], BF16, name="inT", align_bytes=64)
+            else:
+                if kg == 1:
+                    vT[k] = work.tile([128, 2, 256, 4], BF16, name="vT", align_bytes=64, bufs=3)
+                st[k, "q", kg] = vT[k][:, kg - 1, :, :]
+            dst = st[k, "q", kg][:].bitcast(F32) if kg == 0 else st[k, "q", kg].bitcast(F32)
+            src = st[k, "bank", kg][:].rearrange("p u n -> p n u")
+            if on_vector:
+                nc.vector.tensor_copy(out=dst, in_=src)
+            else:
+                nc.scalar.copy(out=dst, in_=src)
+
+        def cat_quantize(k, kg):
+            if (k, "cc") not in st:
+                st[k, "cc"] = work.tile([128, 3, 256], I32, name="cc", align_bytes=64)
+                st[k, "cs"] = work.tile([128, 3, 256], U8, name="cs", align_bytes=64)
+            src = st[k, "q", kg][:] if kg == 0 else st[k, "q", kg]
+            nc.vector.quantize_mx(out=st[k, "cc"][:, kg, :].bitcast(FP8X4), scales=st[k, "cs"][:, kg, :], in_=src.rearrange("p n t -> p (n t)"))
+
+        def widen(k, j):
+            x = work.tile([128, 512], BF16, name="xw", bufs=4)
+            nc.vector.tensor_tensor(out=x[:], in0=xb[k][:, j, :].bitcast(FP8), in1=scl[:], op=ALU.mult)
+            st[k, "x", j] = x
+
+        def h_matmul(k, j, n):
+            acc = psum.tile([128, 512], F32, name="hp")
+            for kg in (1, 2, 0):
+                nc.tensor.matmul_mx(
+                    out=acc[:],
+                    lhsT=st[k, "cc"][:, kg, 128 * j : 128 * j + 128].bitcast(FP8X4),
+                    lhsT_scale=st[k, "cs"][:, kg, 128 * j : 128 * j + 128],
+                    rhs=w1w[kg][:, 512 * n : 512 * n + 512].bitcast(FP8X4),
+                    rhs_scale=w1s[4 * kg : 128, 512 * n : 512 * n + 512],
+                    start=(kg == 1), stop=(kg == 0))
+            st[k, "hp", j, n] = acc
+
+        def h_add(k, j, n):
+            if n == 0:
+                st[k, "hb", j] = work.tile([128, 1024], BF16, name="hb")
+            cols = slice(512 * n, 512 * n + 512)
+            nc.vector.tensor_tensor(out=st[k, "hb", j][:, cols], in0=st[k, "hp", j, n][:], in1=b1c[:, cols], op=ALU.add)
+
+        def h_words(k, j):
+            bank = psum.tile([128, 4, 128], F32, name="wT")
+            words = st[k, "hb", j][:].bitcast(F32)
+            for g in range(2):
+                for u in range(2):
+                    nc.tensor.transpose(bank[:, 2 * g + u, :], words[:, 256 * g + u : 256 * g + 256 : 2], ident[:])
+            st[k, "hbank", j] = bank
+
+        def h_copy(k, j):
+            hT = work.tile([128, 2, 128, 4], BF16, name="hT", align_bytes=64)
+            nc.scalar.copy(out=hT[:].bitcast(F32), in_=st[k, "hbank", j][:].rearrange("p (g u) n -> p g n u", g=2))
+            st[k, "hT", j] = hT
+
+        def h_quantize(k, j):
+            if j == 0:
+                st[k, "hc"] = work.tile([128, 2, 256], I32, name="hc", align_bytes=64)
+                st[k, "hs"] = work.tile([128, 2, 256], U8, name="hs", align_bytes=64)
+            for g in range(2):
+                nc.vector.quantize_mx(
+                    out=st[k, "hc"][:, g, 128 * j : 128 * j + 128].bitcast(FP8X4),
+                    scales=st[k, "hs"][:, g, 128 * j : 128 * j + 128],
+                    in_=st[k, "hT", j][:, g, :, :].rearrange("p n t -> p (n t)"))
+
+        def pre_matmul(k, g):
+            acc = psum.tile([128, 2, 256], F32, name="pp")
+            for u in range(2):
+                cols = slice(256 * g + 128 * u, 256 * g + 128 * u + 128)
+                for kg in range(2):
+                    nc.tensor.matmul_mx(
+                        out=acc[:, u, :],
+                        lhsT=w2p[:, kg, cols].bitcast(FP8X4), lhsT_scale=w2sp[4 * kg : 128, cols],
+                        rhs=st[k, "hc"][:, kg, :].bitcast(FP8X4), rhs_scale=st[k, "hs"][:, kg, :],
+                        start=(kg == 0), stop=(kg == 1))
+            st[k, "pp", g] = acc
+
+        def pre_copy(k, idx):
+            if idx == 0:
+                st[k, "pm"] = work.tile([128, 8, 256], F32, name="pm")
+            nc.scalar.activation(
+                out=st[k, "pm"][:, idx, :], in_=st[k, "pp", idx // 4][:, (idx % 4) // 2, :], func=ACT.Identity,
+                scale=icpm[:].rearrange("p q e -> p (q e)")[:, idx : idx + 1], bias=pbias[:].rearrange("p q e -> p (q e)")[:, idx : idx + 1])
+
+        def sigmoids(k, idx):
+            g, t = idx // 4, idx % 4
+            s0 = work.tile([128, 256], F32, name="s0", bufs=4)
+            s1 = work.tile([128, 256], F32, name="s1", bufs=4)
+            nc.scalar.activation(out=s0[:], in_=vT[k][:, g, :, t], func=ACT.Sigmoid, scale=stdf[:, 2 * idx : 2 * idx + 1], bias=sbias[:, 2 * idx : 2 * idx + 1])
+            nc.scalar.activation(out=s1[:], in_=vT[k][:, g, :, t ^ 1], func=ACT.Sigmoid, scale=stdf[:, 2 * idx + 1 : 2 * idx + 2], bias=sbias[:, 2 * idx + 1 : 2 * idx + 2])
+            st[k, "s", idx] = (s0, s1)
+
+        def conductances(k, idx):
+            s0, s1 = st[k, "s", idx]
+            nabf = nab[:].rearrange("p i c -> p (i c)")
+            nc.scalar.activation(out=s0[:], in_=s0[:], func=ACT.Identity, scale=nabf[:, 2 * idx : 2 * idx + 1], bias=1.0)
+            nc.scalar.activation(out=s1[:], in_=s1[:], func=ACT.Copy, scale=nabf[:, 2 * idx + 1 : 2 * idx + 2])
+
+        def currents(k, idx):
+            g, t = idx // 4, idx % 4
+            if idx == 0:
+                P0[k] = work.tile([128, 8, 256], F32, name="P0")
+                P1[k] = work.tile([128, 8, 256], F32, name="P1")
+            s0, s1 = st[k, "s", idx]
+            own = vT[k][:, g, :, t]
+            nc.vector.scalar_tensor_tensor(out=P0[k][:, idx, :], in0=own, scalar=exc(idx), in1=s0[:], op0=ALU.subtract, op1=ALU.mult)
+            nc.vector.scalar_tensor_tensor(out=P1[k][:, idx, :], in0=own, scalar=inh(idx), in1=s1[:], op0=ALU.subtract, op1=ALU.mult)
+
+        def sum_terms(i, g):
+            k, j = i // 2, i % 2
+            tok = slice(128 * j, 128 * j + 128)
+            x = psum.tile([128, 512], F32, name=("xp", "xp", "xp", "xp", "xp", "xp", "xp", "pp")[i], bufs=2)
+            for t in range(4):
+                idx = 4 * g + t
+                terms = (P0[k], P1[k], st[k, "pm"])
+                for n in range(3):
+                    nc.tensor.matmul(x[:, 128 * t : 128 * t + 128], lhsT=terms[n][:, idx, tok], rhs=ident[:], is_transpose=True, start=(n == 0), stop=(n == 2))
+            st[i, "xp", g] = x
+
+        def row_stats(i, g):
+            if g == 0:
+                st[i, "stats"] = work.tile([128, 2, 6], F32, name="stats")
+            nc.vector.bn_stats(out=st[i, "stats"][:, g, :], in_=st[i, "xp", g][:])
+
+        def row_aggregate(i):
+            mv = work.tile([128, 2], F32, name="mv")
+            nc.vector.bn_aggr(out=mv[:], in_=st[i, "stats"][:].rearrange("p g s -> p (g s)"))
+            st[i, "mu"] = mv[:, 0:1]
+            row_rstd(i, mv[:, 1:2], 1.0)
+
+        def row_rstd(i, square, factor):
+            ve = work.tile([128, 1], F32, name="ve")
+            rstd = work.tile([128, 1], F32, name="rstd")
+            nc.gpsimd.tensor_scalar(out=ve[:], in0=square, scalar1=factor, scalar2=1e-6, op0=ALU.mult, op1=ALU.add)
+            nc.gpsimd.tensor_tensor(out=rstd[:], in0=ve[:], in1=mhalf[:], op=ALU.pow)
+            st[i, "rstd"] = rstd
+
+        def row_sum(i, g):
+            if g == 0:
+                st[i, "sums"] = work.tile([128, 4], F32, name="sums")
+            junk = work.tile([128, 512], F32, name="junk")
+            nc.scalar.activation(out=junk[:], in_=st[i, "xp", g][:], func=ACT.Copy, accum_out=st[i, "sums"][:, g : g + 1])
+
+        def row_mean(i):
+            mean = work.tile([128, 2], F32, name="mean")
+            total = work.tile([128, 1], F32, name="total")
+            nc.gpsimd.tensor_tensor(out=total[:], in0=st[i, "sums"][:, 0:1], in1=st[i, "sums"][:, 1:2], op=ALU.add)
+            nc.gpsimd.tensor_scalar(out=mean[:, 0:1], in0=total[:], scalar1=-1.0 / 1024.0, scalar2=0.0, op0=ALU.mult, op1=ALU.add)
+            nc.gpsimd.tensor_scalar(out=mean[:, 1:2], in0=total[:], scalar1=1.0 / 1024.0, scalar2=0.0, op0=ALU.mult, op1=ALU.add)
+            st[i, "mu"], st[i, "negmu"] = mean[:, 1:2], mean[:, 0:1]
+
+        def row_square(i, g):
+            junk = work.tile([128, 512], F32, name="junk")
+            nc.scalar.activation(out=junk[:], in_=st[i, "xp", g][:], func=ACT.Square, bias=st[i, "negmu"], accum_out=st[i, "sums"][:, 2 + g : 3 + g])
+
+        def row_variance(i):
+            total = work.tile([128, 1], F32, name="total")
+            nc.gpsimd.tensor_tensor(out=total[:], in0=st[i, "sums"][:, 2:3], in1=st[i, "sums"][:, 3:4], op=ALU.add)
+            row_rstd(i, total[:], 1.0 / 1024.0)
+
+        def row_center(i, g):
+            if g == 0:
+                st[i, "y"] = work.tile([128, 1024], F32, name="y")
+            cols = slice(512 * g, 512 * g + 512)
+            nc.vector.scalar_tensor_tensor(
+                out=st[i, "y"][:, cols].rearrange("p (q t) -> p q t", t=4), in0=st[i, "xp", g][:].rearrange("p (t q) -> p q t", t=4),
+                scalar=st[i, "mu"], in1=gmc[:, cols].rearrange("p (q t) -> p q t", t=4), op0=ALU.subtract, op1=ALU.mult)
+
+        def row_store(i, g):
+            if g == 0:
+                st[i, "o"] = work.tile([128, 1024], F32, name="o")
+            cols = slice(512 * g, 512 * g + 512)
+            o = st[i, "o"]
+            nc.vector.scalar_tensor_tensor(out=o[:, cols], in0=st[i, "y"][:, cols], scalar=st[i, "rstd"][:, 0:1], in1=btc[:, cols], op0=ALU.mult, op1=ALU.add)
+            nc.sync.dma_start(out=out[128 * i : 128 * i + 128, cols], in_=o[:, cols])
+
+        def chain(k):
+            steps = []
+            steps.append([(cat_words, k, 1), (widen, k, 0)])
+            steps.append([(cat_copy, k, 1), (cat_words, k, 2), (widen, k, 1)])
+            steps.append([(cat_copy, k, 2), (cat_words, k, 0), (cat_quantize, k, 1)])
+            steps.append([(cat_copy, k, 0), (cat_quantize, k, 2)])
+            steps.append([(cat_quantize, k, 0), (h_matmul, k, 0, 0)])
+            steps.append([(h_matmul, k, 0, 1), (h_add, k, 0, 0)])
+            steps.append([(h_matmul, k, 1, 0), (h_add, k, 0, 1)])
+            steps.append([(h_words, k, 0), (h_matmul, k, 1, 1), (h_copy, k, 0), (h_add, k, 1, 0)])
+            steps.append([(h_quantize, k, 0), (h_add, k, 1, 1)])
+            steps.append([(h_words, k, 1), (h_copy, k, 1)])
+            steps.append([(h_quantize, k, 1)])
+            steps.append([(pre_matmul, k, 0)])
+            steps.append([(pre_matmul, k, 1), (pre_copy, k, 0), (pre_copy, k, 1)])
+            for idx in (2, 4, 6):
+                steps.append([(pre_copy, k, idx), (pre_copy, k, idx + 1)])
+            return steps
+
+        def norm(i):
+            steps = []
+            steps.append([(sum_terms, i, 0)])
+            if i in (7,):
+                steps.append([(sum_terms, i, 1), (row_sum, i, 0)])
+                steps.append([(row_sum, i, 1), (row_mean, i), (row_square, i, 0), (row_square, i, 1), (row_variance, i)])
+            else:
+                steps.append([(sum_terms, i, 1), (row_stats, i, 0)])
+                steps.append([(row_stats, i, 1), (row_aggregate, i)])
+            steps.append([(row_center, i, 0)])
+            steps.append([(row_center, i, 1), (row_store, i, 0)])
+            steps.append([(row_store, i, 1)])
+            return steps
+
+        def run(step):
+            for call in step:
+                call[0](*call[1:])
+
+        chain_steps = [s for k in range(4) for s in chain(k)]
+        norm_steps = [[s for j in range(2) for s in norm(2 * k + j)] for k in range(4)]
+
+        run([(cat_words, 0, 1)])
+        sigmoid_parameters()
+        run([(cat_copy, 0, 1, True), (cat_words, 0, 2)])
+        current_parameters()
+        spread_scale()
+        run([(cat_copy, 0, 2, True), (widen, 0, 0), (widen, 0, 1)])
+        spread_b1()
+        pre_parameters()
+        chain_steps[0:3] = [[(cat_words, 0, 0), (cat_quantize, 0, 1)]]
+        pops = ((3,) * 8, (2,) * 8, (2,) * 8, (1,) * 8)
+        for k in range(4):
+            normals = norm_steps[k - 1] if k > 0 else []
+            for idx in range(8):
+                sigmoids(k, idx)
+                if idx > 0:
+                    currents(k, idx - 1)
+                elif k > 0:
+                    currents(k - 1, 7)
+                for n in range(pops[k][idx]):
+                    if chain_steps:
+                        run(chain_steps.pop(0))
+                    if k == 0 and idx == 1 and n == 0:
+                        permute_w2(0)
+                        permute_w2(1)
+                        permute_w2_scales()
+                for n in range(2 if idx >= 4 else 1):
+                    if normals:
+                        run(normals.pop(0))
+                conductances(k, idx)
+        currents(3, 7)
+        for s in chain_steps:
+            run(s)
+        for s in norm_steps[3]:
+            run(s)

@@ -24,10 +24,10 @@ def tile_memorylayercell_pa_w8_kernel(
         keep = ctx.enter_context(tc.tile_pool(name="keep", bufs=1))
         work = ctx.enter_context(tc.tile_pool(name="work", bufs=2))
         psum = ctx.enter_context(tc.psum_pool(name="psum", bufs=2))
+        ctx.enter_context(tc.manual_schedule())
 
         pr2 = keep.tile([128, 1024], BF16, name="pr2")
         pr1 = keep.tile([128, 512], BF16, name="pr1")
-        prb = keep.tile([128, 1024], BF16, name="prb")
         prf = keep.tile([128, 512], F32, name="prf")
         sts = [keep.tile([128, 2, 1024], BF16, name="sts%d" % k) for k in range(4)]
         xb = [keep.tile([128, 2, 512], U8, name="xb%d" % k) for k in range(4)]
@@ -38,7 +38,8 @@ def tile_memorylayercell_pa_w8_kernel(
         w2p = keep.tile([128, 2, 512], I32, name="w2p", align_bytes=64)
         w2s = keep.tile([128, 512], U8, name="w2s", align_bytes=64)
         w2sp = keep.tile([128, 512], U8, name="w2sp", align_bytes=64)
-        b1c = keep.tile([128, 1024], BF16, name="b1c")
+        w1p = [keep.tile([128, 1024], I32, name="w1p%d" % k, align_bytes=64) for k in range(3)]
+        w1sp = keep.tile([128, 1024], U8, name="w1sp", align_bytes=64)
         gmc = keep.tile([128, 1024], BF16, name="gmc")
         btc = keep.tile([128, 1024], BF16, name="btc")
         ident = keep.tile([128, 128], F32, name="ident")
@@ -54,40 +55,39 @@ def tile_memorylayercell_pa_w8_kernel(
         def load_rows2(n, src):
             nc.scalar.dma_start(out=pr2[2 * n : 2 * n + 2, :], in_=src.rearrange("(g x) c -> g (x c)", g=2))
 
-        def load_rows1(n, src):
-            nc.scalar.dma_start(out=pr1[2 * n : 2 * n + 2, :], in_=src.rearrange("(g x) -> g x", g=2))
+        def load_rows1(n, src, queue):
+            queue.dma_start(out=pr1[2 * n : 2 * n + 2, :], in_=src.rearrange("(g x) -> g x", g=2))
 
         def load_w1(k):
             nc.sync.dma_start(out=w1w[k][:], in_=W1_words[k].rearrange("p n t -> p (n t)").bitcast(I32))
 
         nc.vector.memset(pr2[:].bitcast(I32), 0)
-        nc.vector.memset(pr1[:].bitcast(I32), 0)
         nc.vector.memset(prf[:], 0.0)
+        nc.vector.memset(pr1[:].bitcast(I32), 0)
+        nc.vector.memset(w1s[:].bitcast(I32), 0)
+        nc.vector.memset(w2s[:].bitcast(I32), 0)
         make_identity(nc, ident[:])
         nc.gpsimd.memset(mhalf[:], -0.5)
-        nc.gpsimd.memset(prb[:].bitcast(I32), 0)
-        nc.gpsimd.memset(w1s[:].bitcast(I32), 0)
-        nc.gpsimd.memset(w2s[:].bitcast(I32), 0)
-        for j in range(2):
-            nc.sync.dma_start(out=sts[0][:, j, :], in_=states[128 * j : 128 * j + 128, :])
+        nc.sync.dma_start(out=sts[0][:, 0, :], in_=states[0:128, :])
         load_rows2(0, std_conductance)
         load_rows2(1, mean_conductance_potential)
-        load_rows1(0, capacitance)
         load_rows2(2, max_conductance)
         nc.sync.dma_start(out=prf[0:1, :], in_=inputs_scale)
         load_bytes(0)
-        load_rows1(1, excitatory_potential)
-        load_rows1(2, inhibitory_potential)
+        nc.sync.dma_start(out=sts[0][:, 1, :], in_=states[128:256, :])
+        load_rows1(0, capacitance, nc.scalar)
+        load_rows1(1, excitatory_potential, nc.scalar)
+        load_rows1(2, inhibitory_potential, nc.scalar)
         load_w1(1)
-        nc.scalar.dma_start(out=prb[0:1, :], in_=b1.unsqueeze(0))
-        nc.scalar.dma_start(out=pr1[6:8, 0:256], in_=b2.rearrange("(g x) -> g x", g=2))
         load_w1(2)
         load_w1(0)
+        load_rows1(3, b1, nc.gpsimd)
+        nc.gpsimd.dma_start(out=pr1[8:10, 0:256], in_=b2.rearrange("(g x) -> g x", g=2))
         for q in range(4):
             nc.sync.dma_start(out=w1s[32 * q : 32 * q + 12, :].bitcast(I32), in_=W1_scales[:, 4 * q : 4 * q + 4, :].bitcast(I32))
         load_states(1)
         load_bytes(1)
-        nc.sync.dma_start(out=w2w[:].rearrange("p k n -> p k n"), in_=W2_words.rearrange("k p n t -> p k (n t)").bitcast(I32))
+        nc.sync.dma_start(out=w2w[:], in_=W2_words.rearrange("k p n t -> p k (n t)").bitcast(I32))
         for q in range(4):
             nc.sync.dma_start(out=w2s[32 * q : 32 * q + 8, :].bitcast(I32), in_=W2_scales[:, 4 * q : 4 * q + 4, :].bitcast(I32))
         for k in range(2, 4):
@@ -98,9 +98,8 @@ def tile_memorylayercell_pa_w8_kernel(
         nc.scalar.activation(out=warm[:], in_=mhalf[:], func=ACT.Sigmoid)
 
         p2 = keep.tile([128, 6, 4, 2], BF16, name="p2")
-        p1 = keep.tile([128, 6, 2, 2], BF16, name="p1")
+        p1 = keep.tile([128, 8, 2, 2], BF16, name="p1")
         pb = keep.tile([128, 2, 2], BF16, name="pb")
-        sel = keep.tile([128, 1], BF16, name="sel")
         stdf = keep.tile([128, 16], F32, name="stdf")
         sbias = keep.tile([128, 16], F32, name="sbias")
         icap = keep.tile([128, 8], F32, name="icap")
@@ -127,8 +126,8 @@ def tile_memorylayercell_pa_w8_kernel(
             for u in range(2):
                 nc.tensor.transpose(bank[:, u, :], pr1[:].bitcast(F32)[:, u::2], ident[:])
             nc.tensor.transpose(bank[:, 2, :], pr1[:].bitcast(F32)[:, 0:128], ident[:])
-            nc.vector.tensor_copy(out=p1[:].rearrange("p r u e -> p r (u e)").bitcast(F32), in_=bank[:, 0:2, 0:6].rearrange("p u r -> p r u"))
-            nc.vector.tensor_copy(out=pb[:].rearrange("p g u -> p (g u)").bitcast(F32), in_=bank[:, 2, 6:8])
+            nc.vector.tensor_copy(out=p1[:].rearrange("p r u e -> p r (u e)").bitcast(F32), in_=bank[:, 0:2, 0:8].rearrange("p u r -> p r u"))
+            nc.vector.tensor_copy(out=pb[:].rearrange("p g u -> p (g u)").bitcast(F32), in_=bank[:, 2, 8:10])
             nc.vector.reciprocal(out=icap[:], in_=flat1(0))
             nc.vector.scalar_tensor_tensor(
                 out=nab[:], in0=p2[:, 4:6, :, :].rearrange("p g t c -> p (g t) c"), scalar=-1.0,
@@ -138,13 +137,6 @@ def tile_memorylayercell_pa_w8_kernel(
             bank = psum.tile([128, 512], F32, name="hp")
             nc.tensor.matmul(bank[:], lhsT=ident[:, 0:1].to_broadcast([128, 128]), rhs=prf[:], start=True, stop=True)
             nc.vector.tensor_copy(out=scl[:], in_=bank[:])
-
-        def spread_b1():
-            nc.vector.tensor_copy(out=sel[:], in_=ident[:, 0:1])
-            for n in range(2):
-                bank = psum.tile([128, 512], F32, name="hp")
-                nc.tensor.matmul(bank[:], lhsT=sel[:].to_broadcast([128, 128]), rhs=prb[:, 512 * n : 512 * n + 512], start=True, stop=True)
-                nc.vector.tensor_copy(out=b1c[:, 512 * n : 512 * n + 512], in_=bank[:])
 
         def pre_parameters():
             icv = icap[:].rearrange("p (q e) -> p q e", e=2)
@@ -160,12 +152,21 @@ def tile_memorylayercell_pa_w8_kernel(
         def inh(idx):
             return p1[:, 4:6, :, :].rearrange("p g u e -> p (g u e)")[:, idx : idx + 1]
 
+        def permute_w1(k):
+            nc.vector.tensor_copy(out=w1p[k][:].rearrange("p (g t m) -> p g m t", g=2, t=4), in_=w1w[k][:].rearrange("p (g m t) -> p g m t", g=2, t=4))
+
+        def permute_w1_scales():
+            nc.vector.tensor_copy(out=w1sp[:].rearrange("p (g t m) -> p g m t", g=2, t=4), in_=w1s[:].rearrange("p (g m t) -> p g m t", g=2, t=4))
+
         def permute_w2(k):
             nc.vector.tensor_copy(out=w2p[:, k, :].rearrange("p (g u m) -> p g m u", g=2, u=2), in_=w2w[:, k, :].rearrange("p (g m u) -> p g m u", g=2, u=2))
 
         def permute_w2_scales():
             nc.vector.tensor_copy(out=w2sp[:].rearrange("p (g u m) -> p g m u", g=2, u=2), in_=w2s[:].rearrange("p (g m u) -> p g m u", g=2, u=2))
 
+        groups = ((0,), (1,), (2,), (3,))
+        rows = [256 * len(pairs) for pairs in groups]
+        home = {k: (n, 256 * pairs.index(k)) for n, pairs in enumerate(groups) for k in pairs}
         vT = {}
         P0 = {}
         P1 = {}
@@ -184,9 +185,10 @@ def tile_memorylayercell_pa_w8_kernel(
             if kg == 0:
                 st[k, "q", 0] = work.tile([128, 256, 4], BF16, name="inT", align_bytes=64)
             else:
-                if kg == 1:
-                    vT[k] = work.tile([128, 2, 256, 4], BF16, name="vT", align_bytes=64, bufs=3)
-                st[k, "q", kg] = vT[k][:, kg - 1, :, :]
+                n, r0 = home[k]
+                if kg == 1 and r0 == 0:
+                    vT[n] = work.tile([128, 2, rows[n], 4], BF16, name="vT", align_bytes=64, bufs=3)
+                st[k, "q", kg] = vT[n][:, kg - 1, r0 : r0 + 256, :]
             dst = st[k, "q", kg][:].bitcast(F32) if kg == 0 else st[k, "q", kg].bitcast(F32)
             src = st[k, "bank", kg][:].rearrange("p u n -> p n u")
             if on_vector:
@@ -206,46 +208,30 @@ def tile_memorylayercell_pa_w8_kernel(
             nc.vector.tensor_tensor(out=x[:], in0=xb[k][:, j, :].bitcast(FP8), in1=scl[:], op=ALU.mult)
             st[k, "x", j] = x
 
-        def h_matmul(k, j, n):
-            acc = psum.tile([128, 512], F32, name="hp")
-            for kg in (1, 2, 0):
-                nc.tensor.matmul_mx(
-                    out=acc[:],
-                    lhsT=st[k, "cc"][:, kg, 128 * j : 128 * j + 128].bitcast(FP8X4),
-                    lhsT_scale=st[k, "cs"][:, kg, 128 * j : 128 * j + 128],
-                    rhs=w1w[kg][:, 512 * n : 512 * n + 512].bitcast(FP8X4),
-                    rhs_scale=w1s[4 * kg : 128, 512 * n : 512 * n + 512],
-                    start=(kg == 1), stop=(kg == 0))
-            st[k, "hp", j, n] = acc
+        def h_matmul(k, j, g):
+            acc = psum.tile([128, 4, 128], F32, name="hp")
+            rows_j = slice(128 * j, 128 * j + 128)
+            for t in range(4):
+                cols = slice(512 * g + 128 * t, 512 * g + 128 * t + 128)
+                for kg in (1, 2, 0):
+                    nc.tensor.matmul_mx(
+                        out=acc[:, t, :],
+                        lhsT=w1p[kg][:, cols].bitcast(FP8X4), lhsT_scale=w1sp[4 * kg : 128, cols],
+                        rhs=st[k, "cc"][:, kg, rows_j].bitcast(FP8X4), rhs_scale=st[k, "cs"][:, kg, rows_j],
+                        start=(kg == 1), stop=(kg == 0))
+            st[k, "hp", j, g] = acc
 
-        def h_add(k, j, n):
-            if n == 0:
-                st[k, "hb", j] = work.tile([128, 1024], BF16, name="hb")
-            cols = slice(512 * n, 512 * n + 512)
-            nc.vector.tensor_tensor(out=st[k, "hb", j][:, cols], in0=st[k, "hp", j, n][:], in1=b1c[:, cols], op=ALU.add)
+        def h_add(k, j, g):
+            if j == 0 and g == 0:
+                st[k, "hT"] = work.tile([128, 2, 256, 4], BF16, name="hT", align_bytes=64)
+            bias = flat1(3)[:, 4 * g : 4 * g + 4].unsqueeze(1).to_broadcast([128, 128, 4])
+            nc.vector.tensor_tensor(out=st[k, "hT"][:, g, 128 * j : 128 * j + 128, :], in0=st[k, "hp", j, g][:].rearrange("p t n -> p n t"), in1=bias, op=ALU.add)
 
-        def h_words(k, j):
-            bank = psum.tile([128, 4, 128], F32, name="wT")
-            words = st[k, "hb", j][:].bitcast(F32)
-            for g in range(2):
-                for u in range(2):
-                    nc.tensor.transpose(bank[:, 2 * g + u, :], words[:, 256 * g + u : 256 * g + 256 : 2], ident[:])
-            st[k, "hbank", j] = bank
-
-        def h_copy(k, j):
-            hT = work.tile([128, 2, 128, 4], BF16, name="hT", align_bytes=64)
-            nc.scalar.copy(out=hT[:].bitcast(F32), in_=st[k, "hbank", j][:].rearrange("p (g u) n -> p g n u", g=2))
-            st[k, "hT", j] = hT
-
-        def h_quantize(k, j):
-            if j == 0:
+        def h_quantize(k, g):
+            if g == 0:
                 st[k, "hc"] = work.tile([128, 2, 256], I32, name="hc", align_bytes=64)
                 st[k, "hs"] = work.tile([128, 2, 256], U8, name="hs", align_bytes=64)
-            for g in range(2):
-                nc.vector.quantize_mx(
-                    out=st[k, "hc"][:, g, 128 * j : 128 * j + 128].bitcast(FP8X4),
-                    scales=st[k, "hs"][:, g, 128 * j : 128 * j + 128],
-                    in_=st[k, "hT", j][:, g, :, :].rearrange("p n t -> p (n t)"))
+            nc.vector.quantize_mx(out=st[k, "hc"][:, g, :].bitcast(FP8X4), scales=st[k, "hs"][:, g, :], in_=st[k, "hT"][:, g, :, :].rearrange("p n t -> p (n t)"))
 
         def pre_matmul(k, g):
             acc = psum.tile([128, 2, 256], F32, name="pp")
@@ -261,15 +247,15 @@ def tile_memorylayercell_pa_w8_kernel(
 
         def pre_copy(k, idx):
             if idx == 0:
-                st[k, "pm"] = work.tile([128, 8, 256], F32, name="pm")
+                st[k, "pm"] = work.tile([128, 8, 256], F32, name="pm", bufs=3)
             nc.scalar.activation(
                 out=st[k, "pm"][:, idx, :], in_=st[k, "pp", idx // 4][:, (idx % 4) // 2, :], func=ACT.Identity,
                 scale=icpm[:].rearrange("p q e -> p (q e)")[:, idx : idx + 1], bias=pbias[:].rearrange("p q e -> p (q e)")[:, idx : idx + 1])
 
         def sigmoids(k, idx):
             g, t = idx // 4, idx % 4
-            s0 = work.tile([128, 256], F32, name="s0", bufs=4)
-            s1 = work.tile([128, 256], F32, name="s1", bufs=4)
+            s0 = work.tile([128, rows[k]], F32, name="s0", bufs=4)
+            s1 = work.tile([128, rows[k]], F32, name="s1", bufs=4)
             nc.scalar.activation(out=s0[:], in_=vT[k][:, g, :, t], func=ACT.Sigmoid, scale=stdf[:, 2 * idx : 2 * idx + 1], bias=sbias[:, 2 * idx : 2 * idx + 1])
             nc.scalar.activation(out=s1[:], in_=vT[k][:, g, :, t ^ 1], func=ACT.Sigmoid, scale=stdf[:, 2 * idx + 1 : 2 * idx + 2], bias=sbias[:, 2 * idx + 1 : 2 * idx + 2])
             st[k, "s", idx] = (s0, s1)
@@ -283,8 +269,8 @@ def tile_memorylayercell_pa_w8_kernel(
         def currents(k, idx):
             g, t = idx // 4, idx % 4
             if idx == 0:
-                P0[k] = work.tile([128, 8, 256], F32, name="P0")
-                P1[k] = work.tile([128, 8, 256], F32, name="P1")
+                P0[k] = work.tile([128, 8, rows[k]], F32, name="P0", bufs=3)
+                P1[k] = work.tile([128, 8, rows[k]], F32, name="P1", bufs=3)
             s0, s1 = st[k, "s", idx]
             own = vT[k][:, g, :, t]
             nc.vector.scalar_tensor_tensor(out=P0[k][:, idx, :], in0=own, scalar=exc(idx), in1=s0[:], op0=ALU.subtract, op1=ALU.mult)
@@ -292,13 +278,15 @@ def tile_memorylayercell_pa_w8_kernel(
 
         def sum_terms(i, g):
             k, j = i // 2, i % 2
+            n, r0 = home[k]
             tok = slice(128 * j, 128 * j + 128)
+            gtok = slice(r0 + 128 * j, r0 + 128 * j + 128)
             x = psum.tile([128, 512], F32, name=("xp", "xp", "xp", "xp", "xp", "xp", "xp", "pp")[i], bufs=2)
             for t in range(4):
                 idx = 4 * g + t
-                terms = (P0[k], P1[k], st[k, "pm"])
-                for n in range(3):
-                    nc.tensor.matmul(x[:, 128 * t : 128 * t + 128], lhsT=terms[n][:, idx, tok], rhs=ident[:], is_transpose=True, start=(n == 0), stop=(n == 2))
+                terms = (P0[n][:, idx, gtok], P1[n][:, idx, gtok], st[k, "pm"][:, idx, tok])
+                for m in range(3):
+                    nc.tensor.matmul(x[:, 128 * t : 128 * t + 128], lhsT=terms[m], rhs=ident[:], is_transpose=True, start=(m == 0), stop=(m == 2))
             st[i, "xp", g] = x
 
         def row_stats(i, g):
@@ -353,82 +341,87 @@ def tile_memorylayercell_pa_w8_kernel(
         def row_store(i, g):
             if g == 0:
                 st[i, "o"] = work.tile([128, 1024], F32, name="o")
-            cols = slice(512 * g, 512 * g + 512)
+            cols = slice(512 * g, 512 * g + 512) if i in (7,) else slice(0, 1024)
             o = st[i, "o"]
+            if i not in (7,) and g == 0:
+                return
             nc.vector.scalar_tensor_tensor(out=o[:, cols], in0=st[i, "y"][:, cols], scalar=st[i, "rstd"][:, 0:1], in1=btc[:, cols], op0=ALU.mult, op1=ALU.add)
             nc.sync.dma_start(out=out[128 * i : 128 * i + 128, cols], in_=o[:, cols])
 
-        def chain(k):
-            steps = []
-            steps.append([(cat_words, k, 1), (widen, k, 0)])
-            steps.append([(cat_copy, k, 1), (cat_words, k, 2), (widen, k, 1)])
-            steps.append([(cat_copy, k, 2), (cat_words, k, 0), (cat_quantize, k, 1)])
-            steps.append([(cat_copy, k, 0), (cat_quantize, k, 2)])
-            steps.append([(cat_quantize, k, 0), (h_matmul, k, 0, 0)])
-            steps.append([(h_matmul, k, 0, 1), (h_add, k, 0, 0)])
-            steps.append([(h_matmul, k, 1, 0), (h_add, k, 0, 1)])
-            steps.append([(h_words, k, 0), (h_matmul, k, 1, 1), (h_copy, k, 0), (h_add, k, 1, 0)])
-            steps.append([(h_quantize, k, 0), (h_add, k, 1, 1)])
-            steps.append([(h_words, k, 1), (h_copy, k, 1)])
-            steps.append([(h_quantize, k, 1)])
-            steps.append([(pre_matmul, k, 0)])
-            steps.append([(pre_matmul, k, 1), (pre_copy, k, 0), (pre_copy, k, 1)])
-            for idx in (2, 4, 6):
-                steps.append([(pre_copy, k, idx), (pre_copy, k, idx + 1)])
-            return steps
+        plan = {}
 
-        def norm(i):
-            steps = []
-            steps.append([(sum_terms, i, 0)])
-            if i in (7,):
-                steps.append([(sum_terms, i, 1), (row_sum, i, 0)])
-                steps.append([(row_sum, i, 1), (row_mean, i), (row_square, i, 0), (row_square, i, 1), (row_variance, i)])
+        def place(kind, slot, *calls):
+            plan.setdefault((slot, kind), []).extend(calls)
+
+        def place_norm(i, s, d):
+            place("norm", s, (sum_terms, i, 0))
+            if i in ():
+                place("norm", s + d[0], (sum_terms, i, 1), (row_sum, i, 0))
+                place("norm", s + d[1], (row_sum, i, 1), (row_mean, i))
+                place("norm", s + d[2], (row_square, i, 0), (row_square, i, 1), (row_variance, i))
             else:
-                steps.append([(sum_terms, i, 1), (row_stats, i, 0)])
-                steps.append([(row_stats, i, 1), (row_aggregate, i)])
-            steps.append([(row_center, i, 0)])
-            steps.append([(row_center, i, 1), (row_store, i, 0)])
-            steps.append([(row_store, i, 1)])
-            return steps
+                place("norm", s + d[0], (sum_terms, i, 1), (row_stats, i, 0))
+                place("norm", s + d[1], (row_stats, i, 1))
+                place("norm", s + d[2], (row_aggregate, i))
+            place("norm", s + d[3], (row_center, i, 0), (row_center, i, 1))
+            place("norm", s + d[4], (row_store, i, 0), (row_store, i, 1))
 
-        def run(step):
-            for call in step:
-                call[0](*call[1:])
+        def place_chain(k, s, d):
+            place("chain", s, (cat_words, k, 1), (widen, k, 0))
+            place("chain", s + d[0], (cat_copy, k, 1), (cat_words, k, 2), (widen, k, 1))
+            place("chain", s + d[1], (cat_copy, k, 2), (cat_words, k, 0), (cat_quantize, k, 1))
+            place("chain", s + d[2], (cat_copy, k, 0), (cat_quantize, k, 2))
+            place("chain", s + d[3], (cat_quantize, k, 0))
 
-        chain_steps = [s for k in range(4) for s in chain(k)]
-        norm_steps = [[s for j in range(2) for s in norm(2 * k + j)] for k in range(4)]
+        def place_rest(k, s, e):
+            order = ((0, 0), (1, 0), (0, 1), (1, 1))
+            for n in range(4):
+                j, g = order[n]
+                place("chain", s + e[2 * n], (h_matmul, k, j, g))
+                place("chain", s + e[2 * n + 1], (h_add, k, j, g))
+                if j == 1:
+                    place("chain", s + e[8 + g], (h_quantize, k, g))
+            place("chain", s + e[10], (pre_matmul, k, 0))
+            place("chain", s + e[11], (pre_copy, k, 0), (pre_copy, k, 1))
+            place("chain", s + e[12], (pre_matmul, k, 1), (pre_copy, k, 2), (pre_copy, k, 3))
+            place("chain", s + e[13], (pre_copy, k, 4), (pre_copy, k, 5))
+            place("chain", s + e[14], (pre_copy, k, 6), (pre_copy, k, 7))
 
-        run([(cat_words, 0, 1)])
-        sigmoid_parameters()
-        run([(cat_copy, 0, 1, True), (cat_words, 0, 2)])
-        current_parameters()
-        spread_scale()
-        run([(cat_copy, 0, 2, True), (widen, 0, 0), (widen, 0, 1)])
-        spread_b1()
-        pre_parameters()
-        chain_steps[0:3] = [[(cat_words, 0, 0), (cat_quantize, 0, 1)]]
-        pops = ((3,) * 8, (2,) * 8, (2,) * 8, (1,) * 8)
+        chain_at = (4, 9, 15)
+        rest_at = (6, 11, 18, 22)
+        norm_at = (16, 19, 22, 25, 28, 31, 37, 33)
+        for i in range(8):
+            place_norm(i, norm_at[i], (1, 1, 3, 3, 4) if i < 6 else (1, 2, 2, 2, 5))
         for k in range(4):
-            normals = norm_steps[k - 1] if k > 0 else []
             for idx in range(8):
-                sigmoids(k, idx)
-                if idx > 0:
-                    currents(k, idx - 1)
-                elif k > 0:
-                    currents(k - 1, 7)
-                for n in range(pops[k][idx]):
-                    if chain_steps:
-                        run(chain_steps.pop(0))
-                    if k == 0 and idx == 1 and n == 0:
-                        permute_w2(0)
-                        permute_w2(1)
-                        permute_w2_scales()
-                for n in range(2 if idx >= 4 else 1):
-                    if normals:
-                        run(normals.pop(0))
-                conductances(k, idx)
-        currents(3, 7)
-        for s in chain_steps:
-            run(s)
-        for s in norm_steps[3]:
-            run(s)
+                place("sigmoid", 8 * k + idx, (sigmoids, k, idx))
+                place("current", 8 * k + idx + 2, (currents, k, idx))
+                place("conduct", 8 * k + idx, (conductances, k, idx))
+            if k > 0:
+                place_chain(k, chain_at[k - 1], (1, 2, 3, 5))
+            place_rest(k, rest_at[k], (0, 1, 1, 2, 2, 3, 3, 4, 3, 5, 6, 7, 8, 9, 10))
+        place("chain", (1, 2, 2, 5, 7)[0], (cat_quantize, 0, 1), (permute_w1, 2))
+        place("chain", (1, 2, 2, 5, 7)[1], (cat_quantize, 0, 2), (cat_words, 0, 0), (permute_w1, 0))
+        place("chain", (1, 2, 2, 5, 7)[2], (cat_copy, 0, 0), (pre_parameters,), (permute_w1_scales,))
+        place("chain", (1, 2, 2, 5, 7)[3], (cat_quantize, 0, 0))
+        place("chain", (1, 2, 2, 5, 7)[4], (permute_w2, 0), (permute_w2, 1), (permute_w2_scales,))
+        cat_words(0, 1)
+        cat_copy(0, 1, True)
+        sigmoid_parameters()
+        spread_scale()
+        cat_words(0, 2)
+        cat_copy(0, 2, True)
+        current_parameters()
+        widen(0, 0)
+        widen(0, 1)
+        permute_w1(1)
+        for slot in range(0, max(key[0] for key in plan) + 1):
+            lists = [plan.get((slot, kind), []) for kind in ("norm", "current", "chain")]
+            for call in plan.get((slot, "sigmoid"), []):
+                call[0](*call[1:])
+            for n in range(max(len(calls) for calls in lists)):
+                for calls in lists:
+                    if n < len(calls):
+                        calls[n][0](*calls[n][1:])
+            for call in plan.get((slot, "conduct"), []):
+                call[0](*call[1:])

@@ -27,7 +27,9 @@ def tile_memorylayercell_pa_w8_kernel(
         ctx.enter_context(tc.manual_schedule())
 
         pr2 = keep.tile([128, 1024], BF16, name="pr2")
+        prm = keep.tile([128, 1024], BF16, name="prm")
         pr1 = keep.tile([128, 512], BF16, name="pr1")
+        prb = keep.tile([128, 512], BF16, name="prb")
         prf = keep.tile([128, 512], F32, name="prf")
         sts = [keep.tile([128, 2, 1024], BF16, name="sts%d" % k) for k in range(4)]
         xb = [keep.tile([128, 2, 512], U8, name="xb%d" % k) for k in range(4)]
@@ -52,37 +54,39 @@ def tile_memorylayercell_pa_w8_kernel(
         def load_bytes(k):
             nc.sync.dma_start(out=xb[k][:], in_=inputs_bytes[256 * k : 256 * k + 256, :].rearrange("(i p) k -> p i k", p=128))
 
-        def load_rows2(n, src):
-            nc.scalar.dma_start(out=pr2[2 * n : 2 * n + 2, :], in_=src.rearrange("(g x) c -> g (x c)", g=2))
+        def load_rows2(dst, n, src):
+            nc.scalar.dma_start(out=dst[2 * n : 2 * n + 2, :], in_=src.rearrange("(g x) c -> g (x c)", g=2))
 
-        def load_rows1(n, src, queue):
-            queue.dma_start(out=pr1[2 * n : 2 * n + 2, :], in_=src.rearrange("(g x) -> g x", g=2))
+        def load_rows1(dst, n, src, queue):
+            queue.dma_start(out=dst[2 * n : 2 * n + 2, :], in_=src.rearrange("(g x) -> g x", g=2))
 
         def load_w1(k):
             nc.sync.dma_start(out=w1w[k][:], in_=W1_words[k].rearrange("p n t -> p (n t)").bitcast(I32))
 
         nc.vector.memset(pr2[:].bitcast(I32), 0)
         nc.vector.memset(prf[:], 0.0)
+        nc.vector.memset(prm[:].bitcast(I32), 0)
         nc.vector.memset(pr1[:].bitcast(I32), 0)
         nc.vector.memset(w1s[:].bitcast(I32), 0)
         nc.vector.memset(w2s[:].bitcast(I32), 0)
         make_identity(nc, ident[:])
         nc.gpsimd.memset(mhalf[:], -0.5)
+        nc.gpsimd.memset(prb[:].bitcast(I32), 0)
         nc.sync.dma_start(out=sts[0][:, 0, :], in_=states[0:128, :])
-        load_rows2(0, std_conductance)
-        load_rows2(1, mean_conductance_potential)
-        load_rows2(2, max_conductance)
+        load_rows2(pr2, 0, std_conductance)
+        load_rows2(pr2, 1, mean_conductance_potential)
+        nc.sync.dma_start(out=sts[0][:, 1, :], in_=states[128:256, :])
+        load_rows2(prm, 0, max_conductance)
+        load_rows1(pr1, 0, capacitance, nc.scalar)
+        load_rows1(pr1, 1, excitatory_potential, nc.scalar)
+        load_rows1(pr1, 2, inhibitory_potential, nc.scalar)
         nc.sync.dma_start(out=prf[0:1, :], in_=inputs_scale)
         load_bytes(0)
-        nc.sync.dma_start(out=sts[0][:, 1, :], in_=states[128:256, :])
-        load_rows1(0, capacitance, nc.scalar)
-        load_rows1(1, excitatory_potential, nc.scalar)
-        load_rows1(2, inhibitory_potential, nc.scalar)
         load_w1(1)
         load_w1(2)
         load_w1(0)
-        load_rows1(3, b1, nc.gpsimd)
-        nc.gpsimd.dma_start(out=pr1[8:10, 0:256], in_=b2.rearrange("(g x) -> g x", g=2))
+        load_rows1(prb, 0, b1, nc.gpsimd)
+        nc.gpsimd.dma_start(out=prb[2:4, 0:256], in_=b2.rearrange("(g x) -> g x", g=2))
         for q in range(4):
             nc.sync.dma_start(out=w1s[32 * q : 32 * q + 12, :].bitcast(I32), in_=W1_scales[:, 4 * q : 4 * q + 4, :].bitcast(I32))
         load_states(1)
@@ -97,8 +101,10 @@ def tile_memorylayercell_pa_w8_kernel(
         nc.sync.dma_start(out=btc[:], in_=beta.partition_broadcast(128))
         nc.scalar.activation(out=warm[:], in_=mhalf[:], func=ACT.Sigmoid)
 
-        p2 = keep.tile([128, 6, 4, 2], BF16, name="p2")
-        p1 = keep.tile([128, 8, 2, 2], BF16, name="p1")
+        p2 = keep.tile([128, 4, 4, 2], BF16, name="p2")
+        pm2 = keep.tile([128, 2, 4, 2], BF16, name="pm2")
+        pq = keep.tile([128, 2, 2, 2], BF16, name="pq")
+        p1 = keep.tile([128, 6, 2, 2], BF16, name="p1")
         pb = keep.tile([128, 2, 2], BF16, name="pb")
         stdf = keep.tile([128, 16], F32, name="stdf")
         sbias = keep.tile([128, 16], F32, name="sbias")
@@ -117,21 +123,31 @@ def tile_memorylayercell_pa_w8_kernel(
             bank = psum.tile([128, 4, 128], F32, name="wT")
             for t in range(4):
                 nc.tensor.transpose(bank[:, t, :], pr2[:].bitcast(F32)[:, t::4], ident[:])
-            nc.vector.tensor_copy(out=p2[:].rearrange("p r t c -> p r (t c)").bitcast(F32), in_=bank[:, :, 0:6].rearrange("p t r -> p r t"))
+            nc.vector.tensor_copy(out=p2[:].rearrange("p r t c -> p r (t c)").bitcast(F32), in_=bank[:, :, 0:4].rearrange("p t r -> p r t"))
             nc.vector.tensor_copy(out=stdf[:], in_=flat2(0))
             nc.vector.scalar_tensor_tensor(out=sbias[:], in0=flat2(1), scalar=-1.0, in1=flat2(0), op0=ALU.mult, op1=ALU.mult)
 
         def current_parameters():
-            bank = psum.tile([128, 4, 128], F32, name="wT")
+            bank = psum.tile([128, 4, 128], F32, name="hp")
+            for t in range(4):
+                nc.tensor.transpose(bank[:, t, :], prm[:].bitcast(F32)[:, t::4], ident[:])
+            nc.vector.tensor_copy(out=pm2[:].rearrange("p r t c -> p r (t c)").bitcast(F32), in_=bank[:, :, 0:2].rearrange("p t r -> p r t"))
+            bank = psum.tile([128, 4, 128], F32, name="hp")
             for u in range(2):
                 nc.tensor.transpose(bank[:, u, :], pr1[:].bitcast(F32)[:, u::2], ident[:])
-            nc.tensor.transpose(bank[:, 2, :], pr1[:].bitcast(F32)[:, 0:128], ident[:])
-            nc.vector.tensor_copy(out=p1[:].rearrange("p r u e -> p r (u e)").bitcast(F32), in_=bank[:, 0:2, 0:8].rearrange("p u r -> p r u"))
-            nc.vector.tensor_copy(out=pb[:].rearrange("p g u -> p (g u)").bitcast(F32), in_=bank[:, 2, 8:10])
+            nc.vector.tensor_copy(out=p1[:].rearrange("p r u e -> p r (u e)").bitcast(F32), in_=bank[:, 0:2, 0:6].rearrange("p u r -> p r u"))
             nc.vector.reciprocal(out=icap[:], in_=flat1(0))
             nc.vector.scalar_tensor_tensor(
-                out=nab[:], in0=p2[:, 4:6, :, :].rearrange("p g t c -> p (g t) c"), scalar=-1.0,
+                out=nab[:], in0=pm2[:].rearrange("p g t c -> p (g t) c"), scalar=-1.0,
                 in1=icap[:].unsqueeze(2).to_broadcast([128, 8, 2]), op0=ALU.mult, op1=ALU.mult)
+
+        def bias_parameters():
+            bank = psum.tile([128, 4, 128], F32, name="hp")
+            for u in range(2):
+                nc.tensor.transpose(bank[:, u, :], prb[:].bitcast(F32)[:, u::2], ident[:])
+            nc.tensor.transpose(bank[:, 2, :], prb[:].bitcast(F32)[:, 0:128], ident[:])
+            nc.vector.tensor_copy(out=pq[:].rearrange("p r u e -> p r (u e)").bitcast(F32), in_=bank[:, 0:2, 0:2].rearrange("p u r -> p r u"))
+            nc.vector.tensor_copy(out=pb[:].rearrange("p g u -> p (g u)").bitcast(F32), in_=bank[:, 2, 2:4])
 
         def spread_scale():
             bank = psum.tile([128, 512], F32, name="hp")
@@ -224,7 +240,7 @@ def tile_memorylayercell_pa_w8_kernel(
         def h_add(k, j, g):
             if j == 0 and g == 0:
                 st[k, "hT"] = work.tile([128, 2, 256, 4], BF16, name="hT", align_bytes=64)
-            bias = flat1(3)[:, 4 * g : 4 * g + 4].unsqueeze(1).to_broadcast([128, 128, 4])
+            bias = pq[:].rearrange("p g u e -> p (g u e)")[:, 4 * g : 4 * g + 4].unsqueeze(1).to_broadcast([128, 128, 4])
             nc.vector.tensor_tensor(out=st[k, "hT"][:, g, 128 * j : 128 * j + 128, :], in0=st[k, "hp", j, g][:].rearrange("p t n -> p n t"), in1=bias, op=ALU.add)
 
         def h_quantize(k, g):
@@ -281,7 +297,7 @@ def tile_memorylayercell_pa_w8_kernel(
             n, r0 = home[k]
             tok = slice(128 * j, 128 * j + 128)
             gtok = slice(r0 + 128 * j, r0 + 128 * j + 128)
-            x = psum.tile([128, 512], F32, name=("xp", "xp", "xp", "xp", "xp", "xp", "xp", "pp")[i], bufs=2)
+            x = psum.tile([128, 512], F32, name=("xp", "xp", "xp", "xp", "xp", "hp", "xp", "pp")[i], bufs=2)
             for t in range(4):
                 idx = 4 * g + t
                 terms = (P0[n][:, idx, gtok], P1[n][:, idx, gtok], st[k, "pm"][:, idx, tok])
@@ -355,7 +371,7 @@ def tile_memorylayercell_pa_w8_kernel(
 
         def place_norm(i, s, d):
             place("norm", s, (sum_terms, i, 0))
-            if i in ():
+            if i in (5, 7):
                 place("norm", s + d[0], (sum_terms, i, 1), (row_sum, i, 0))
                 place("norm", s + d[1], (row_sum, i, 1), (row_mean, i))
                 place("norm", s + d[2], (row_square, i, 0), (row_square, i, 1), (row_variance, i))
@@ -387,31 +403,31 @@ def tile_memorylayercell_pa_w8_kernel(
             place("chain", s + e[13], (pre_copy, k, 4), (pre_copy, k, 5))
             place("chain", s + e[14], (pre_copy, k, 6), (pre_copy, k, 7))
 
-        chain_at = (4, 9, 15)
-        rest_at = (6, 11, 18, 22)
-        norm_at = (16, 19, 22, 25, 28, 31, 37, 33)
+        chain_at = (4, 8, 15)
+        rest_at = (6, 11, 17, 20)
+        norm_at = (16, 19, 22, 25, 29, 31, 36, 40)
         for i in range(8):
-            place_norm(i, norm_at[i], (1, 1, 3, 3, 4) if i < 6 else (1, 2, 2, 2, 5))
+            place_norm(i, norm_at[i], (2, 2, 3, 3, 7) if i in (5, 7) else (1, 1, 2, 3, 4) if i < 6 else (1, 4, 4, 4, 4))
         for k in range(4):
             for idx in range(8):
                 place("sigmoid", 8 * k + idx, (sigmoids, k, idx))
-                place("current", 8 * k + idx + 2, (currents, k, idx))
+                place("current", 8 * k + idx + 3, (currents, k, idx))
                 place("conduct", 8 * k + idx, (conductances, k, idx))
             if k > 0:
-                place_chain(k, chain_at[k - 1], (1, 2, 3, 5))
-            place_rest(k, rest_at[k], (0, 1, 1, 2, 2, 3, 3, 4, 3, 5, 6, 7, 8, 9, 10))
-        place("chain", (1, 2, 2, 5, 7)[0], (cat_quantize, 0, 1), (permute_w1, 2))
-        place("chain", (1, 2, 2, 5, 7)[1], (cat_quantize, 0, 2), (cat_words, 0, 0), (permute_w1, 0))
-        place("chain", (1, 2, 2, 5, 7)[2], (cat_copy, 0, 0), (pre_parameters,), (permute_w1_scales,))
-        place("chain", (1, 2, 2, 5, 7)[3], (cat_quantize, 0, 0))
-        place("chain", (1, 2, 2, 5, 7)[4], (permute_w2, 0), (permute_w2, 1), (permute_w2_scales,))
+                place_chain(k, chain_at[k - 1], (1, 2, 4, 5))
+            place_rest(k, rest_at[k], (0, 1, 1, 2, 2, 3, 3, 4, 3, 5, 6, 7, 8, 9, 8))
+        place("chain", (3, 1, 2, 5, 5)[0], (cat_quantize, 0, 1), (permute_w1, 2))
+        place("chain", (3, 1, 2, 5, 5)[1], (cat_quantize, 0, 2), (cat_words, 0, 0), (permute_w1, 0))
+        place("chain", (3, 1, 2, 5, 5)[2], (cat_copy, 0, 0), (bias_parameters,), (pre_parameters,), (permute_w1_scales,))
+        place("chain", (3, 1, 2, 5, 5)[3], (cat_quantize, 0, 0))
+        place("chain", (3, 1, 2, 5, 5)[4], (permute_w2, 0), (permute_w2, 1), (permute_w2_scales,))
         cat_words(0, 1)
         cat_copy(0, 1, True)
         sigmoid_parameters()
-        spread_scale()
+        current_parameters()
         cat_words(0, 2)
         cat_copy(0, 2, True)
-        current_parameters()
+        spread_scale()
         widen(0, 0)
         widen(0, 1)
         permute_w1(1)

@@ -14,6 +14,26 @@ ACT = mybir.ActivationFunctionType
 
 FLOPS = 2 * 1024 * (1536 * 1024 + 1024 * 512)
 
+P = 128
+SETS = 8
+PAIRS = 4
+PAIR = 2 * P
+EPS = 1e-6
+
+CAT_START = (4, 8, 12)
+CAT_STEPS = (2, 3, 4, 6)
+PRODUCT_START = (6, 11, 16, 20)
+PRODUCT_STEPS = (0, 1, 1, 2, 2, 3, 3, 4, 5, 6, 7, 8, 9, 9)
+CURRENT_STEP = 2
+NORM_START = (15, 18, 22, 24, 27, 29, 33, 36)
+NORM_STEPS = (1, 2, 2, 3, 4)
+LAST_NORM_STEPS = (0, 1, 3, 3, 8)
+SCALAR_NORM_STEPS = (1, 2, 3, 5, 7)
+HEAD = (1, 1, 2, 3, 2, 4, 1, 3, 4, 7)
+
+SCALAR_STATS = (3, 5, 7)
+X_BANKS = ("x", "x", "x", "words", "x", "words", "h_sums", "pre_sums")
+
 
 def tile_memorylayercell_pa_w8_kernel(
     tc, inputs_bytes, inputs_scale, states, W1_words, W1_scales, b1, W2_words, W2_scales, b2,
@@ -26,418 +46,406 @@ def tile_memorylayercell_pa_w8_kernel(
         psum = ctx.enter_context(tc.psum_pool(name="psum", bufs=2))
         ctx.enter_context(tc.manual_schedule())
 
-        pr2 = keep.tile([128, 1024], BF16, name="pr2")
-        prm = keep.tile([128, 1024], BF16, name="prm")
-        pr1 = keep.tile([128, 512], BF16, name="pr1")
-        prb = keep.tile([128, 512], BF16, name="prb")
-        prf = keep.tile([128, 512], F32, name="prf")
-        sts = [keep.tile([128, 2, 1024], BF16, name="sts%d" % k) for k in range(4)]
-        xb = [keep.tile([128, 2, 512], U8, name="xb%d" % k) for k in range(4)]
-        scl = keep.tile([128, 512], F32, name="scl")
-        w1w = [keep.tile([128, 1024], I32, name="w1w%d" % k, align_bytes=64) for k in range(3)]
-        w1s = keep.tile([128, 1024], U8, name="w1s", align_bytes=64)
-        w2w = keep.tile([128, 2, 512], I32, name="w2w", align_bytes=64)
-        w2p = keep.tile([128, 2, 512], I32, name="w2p", align_bytes=64)
-        w2s = keep.tile([128, 512], U8, name="w2s", align_bytes=64)
-        w2sp = keep.tile([128, 512], U8, name="w2sp", align_bytes=64)
-        w1p = [keep.tile([128, 1024], I32, name="w1p%d" % k, align_bytes=64) for k in range(3)]
-        w1sp = keep.tile([128, 1024], U8, name="w1sp", align_bytes=64)
-        gmc = keep.tile([128, 1024], BF16, name="gmc")
-        btc = keep.tile([128, 1024], BF16, name="btc")
-        ident = keep.tile([128, 128], F32, name="ident")
-        mhalf = keep.tile([128, 1], F32, name="mhalf")
-        warm = keep.tile([128, 1], F32, name="warm")
+        slope_rows = keep.tile([P, 1024], BF16, name="slope_rows")
+        max_rows = keep.tile([P, 1024], BF16, name="max_rows")
+        cell_rows = keep.tile([P, 512], BF16, name="cell_rows")
+        bias_rows = keep.tile([P, 512], BF16, name="bias_rows")
+        scale_row = keep.tile([P, 512], F32, name="scale_row")
+        state_rows = [keep.tile([P, 2, 1024], BF16, name="state_rows%d" % k) for k in range(PAIRS)]
+        input_bytes = [keep.tile([P, 2, 512], U8, name="input_bytes%d" % k) for k in range(PAIRS)]
+        input_scale = keep.tile([P, 512], F32, name="input_scale")
+        w1_words = [keep.tile([P, 1024], I32, name="w1_words%d" % kg, align_bytes=64) for kg in range(3)]
+        w1_scales = keep.tile([P, 1024], U8, name="w1_scales", align_bytes=64)
+        w2_words = keep.tile([P, 2, 512], I32, name="w2_words", align_bytes=64)
+        w2_turned = keep.tile([P, 2, 512], I32, name="w2_turned", align_bytes=64)
+        w2_scales = keep.tile([P, 512], U8, name="w2_scales", align_bytes=64)
+        w2_scales_turned = keep.tile([P, 512], U8, name="w2_scales_turned", align_bytes=64)
+        w1_turned = [keep.tile([P, 1024], I32, name="w1_turned%d" % kg, align_bytes=64) for kg in range(3)]
+        w1_scales_turned = keep.tile([P, 1024], U8, name="w1_scales_turned", align_bytes=64)
+        gamma_all = keep.tile([P, 1024], BF16, name="gamma_all")
+        beta_all = keep.tile([P, 1024], BF16, name="beta_all")
+        ident = keep.tile([P, P], F32, name="ident")
+        minus_half = keep.tile([P, 1], F32, name="minus_half")
+        warm = keep.tile([P, 1], F32, name="warm")
+
+        slopes = keep.tile([P, 4, 4, 2], BF16, name="slopes")
+        maxima = keep.tile([P, 2, 4, 2], BF16, name="maxima")
+        b1_col = keep.tile([P, 2, 2, 2], BF16, name="b1_col")
+        cells = keep.tile([P, 6, 2, 2], BF16, name="cells")
+        b2_col = keep.tile([P, 2, 2], BF16, name="b2_col")
+        std_col = keep.tile([P, 16], F32, name="std_col")
+        sigmoid_bias = keep.tile([P, 16], F32, name="sigmoid_bias")
+        inv_cap = keep.tile([P, SETS], F32, name="inv_cap")
+        minus_ab = keep.tile([P, SETS, 2], F32, name="minus_ab")
+        pre_scale = keep.tile([P, 4, 2], F32, name="pre_scale")
+        pre_bias = keep.tile([P, 4, 2], F32, name="pre_bias")
 
         def load_states(k):
-            nc.sync.dma_start(out=sts[k][:], in_=states[256 * k : 256 * k + 256, :].rearrange("(i p) s -> p i s", p=128))
+            nc.sync.dma_start(out=state_rows[k][:], in_=states[PAIR * k : PAIR * k + PAIR, :].rearrange("(i p) s -> p i s", p=P))
 
         def load_bytes(k):
-            nc.sync.dma_start(out=xb[k][:], in_=inputs_bytes[256 * k : 256 * k + 256, :].rearrange("(i p) k -> p i k", p=128))
+            nc.sync.dma_start(out=input_bytes[k][:], in_=inputs_bytes[PAIR * k : PAIR * k + PAIR, :].rearrange("(i p) k -> p i k", p=P))
 
-        def load_rows2(dst, n, src):
-            nc.scalar.dma_start(out=dst[2 * n : 2 * n + 2, :], in_=src.rearrange("(g x) c -> g (x c)", g=2))
+        def load_conductance(dst, n, src):
+            nc.sync.dma_start(out=dst[2 * n : 2 * n + 2, :], in_=src.rearrange("(g x) c -> g (x c)", g=2))
 
-        def load_rows1(dst, n, src, queue):
+        def load_vector(dst, n, src, queue):
             queue.dma_start(out=dst[2 * n : 2 * n + 2, :], in_=src.rearrange("(g x) -> g x", g=2))
 
-        def load_w1(k):
-            nc.sync.dma_start(out=w1w[k][:], in_=W1_words[k].rearrange("p n t -> p (n t)").bitcast(I32))
+        nc.vector.memset(warm[:], 0.0)
+        nc.scalar.activation(out=warm[:], in_=warm[:], func=ACT.Sigmoid)
 
-        nc.vector.memset(pr2[:].bitcast(I32), 0)
-        nc.vector.memset(prf[:], 0.0)
-        nc.vector.memset(prm[:].bitcast(I32), 0)
-        nc.vector.memset(pr1[:].bitcast(I32), 0)
-        nc.vector.memset(w1s[:].bitcast(I32), 0)
-        nc.vector.memset(w2s[:].bitcast(I32), 0)
+        nc.vector.memset(slope_rows[:].bitcast(I32), 0)
+        nc.vector.memset(scale_row[:], 0.0)
+        nc.vector.memset(max_rows[:].bitcast(I32), 0)
+        nc.vector.memset(cell_rows[:].bitcast(I32), 0)
+        nc.vector.memset(w1_scales[:].bitcast(I32), 0)
+        nc.vector.memset(w2_scales[:].bitcast(I32), 0)
         make_identity(nc, ident[:])
-        nc.gpsimd.memset(mhalf[:], -0.5)
-        nc.gpsimd.memset(prb[:].bitcast(I32), 0)
-        nc.sync.dma_start(out=sts[0][:, 0, :], in_=states[0:128, :])
-        load_rows2(pr2, 0, std_conductance)
-        load_rows2(pr2, 1, mean_conductance_potential)
-        nc.sync.dma_start(out=sts[0][:, 1, :], in_=states[128:256, :])
-        load_rows2(prm, 0, max_conductance)
-        load_rows1(pr1, 0, capacitance, nc.scalar)
-        load_rows1(pr1, 1, excitatory_potential, nc.scalar)
-        load_rows1(pr1, 2, inhibitory_potential, nc.scalar)
-        nc.sync.dma_start(out=prf[0:1, :], in_=inputs_scale)
+        nc.gpsimd.memset(minus_half[:], -0.5)
+        nc.gpsimd.memset(bias_rows[:].bitcast(I32), 0)
+
+        nc.sync.dma_start(out=state_rows[0][:, 0, :], in_=states[0:P, :])
+        load_conductance(slope_rows, 0, std_conductance)
+        load_conductance(slope_rows, 1, mean_conductance_potential)
+        nc.sync.dma_start(out=state_rows[0][:, 1, :], in_=states[P:PAIR, :])
+        load_conductance(max_rows, 0, max_conductance)
+        load_vector(cell_rows, 0, capacitance, nc.sync)
+        load_vector(cell_rows, 1, excitatory_potential, nc.sync)
+        load_vector(cell_rows, 2, inhibitory_potential, nc.sync)
+        nc.sync.dma_start(out=scale_row[0:1, :], in_=inputs_scale)
         load_bytes(0)
-        load_w1(1)
-        load_w1(2)
-        load_w1(0)
-        load_rows1(prb, 0, b1, nc.gpsimd)
-        nc.gpsimd.dma_start(out=prb[2:4, 0:256], in_=b2.rearrange("(g x) -> g x", g=2))
+        for kg in (1, 2, 0):
+            nc.sync.dma_start(out=w1_words[kg][:], in_=W1_words[kg].rearrange("p n t -> p (n t)").bitcast(I32))
         for q in range(4):
-            nc.sync.dma_start(out=w1s[32 * q : 32 * q + 12, :].bitcast(I32), in_=W1_scales[:, 4 * q : 4 * q + 4, :].bitcast(I32))
+            nc.sync.dma_start(out=w1_scales[32 * q : 32 * q + 12, :].bitcast(I32), in_=W1_scales[:, 4 * q : 4 * q + 4, :].bitcast(I32))
+        load_vector(bias_rows, 0, b1, nc.gpsimd)
+        nc.gpsimd.dma_start(out=bias_rows[2:4, 0:256], in_=b2.rearrange("(g x) -> g x", g=2))
         load_states(1)
         load_bytes(1)
-        nc.sync.dma_start(out=w2w[:], in_=W2_words.rearrange("k p n t -> p k (n t)").bitcast(I32))
+        nc.sync.dma_start(out=w2_words[:], in_=W2_words.rearrange("k p n t -> p k (n t)").bitcast(I32))
         for q in range(4):
-            nc.sync.dma_start(out=w2s[32 * q : 32 * q + 8, :].bitcast(I32), in_=W2_scales[:, 4 * q : 4 * q + 4, :].bitcast(I32))
-        for k in range(2, 4):
+            nc.sync.dma_start(out=w2_scales[32 * q : 32 * q + 8, :].bitcast(I32), in_=W2_scales[:, 4 * q : 4 * q + 4, :].bitcast(I32))
+        for k in range(2, PAIRS):
             load_states(k)
             load_bytes(k)
-        nc.sync.dma_start(out=gmc[:], in_=gamma.partition_broadcast(128))
-        nc.sync.dma_start(out=btc[:], in_=beta.partition_broadcast(128))
-        nc.scalar.activation(out=warm[:], in_=mhalf[:], func=ACT.Sigmoid)
+        nc.sync.dma_start(out=gamma_all[:], in_=gamma.partition_broadcast(P))
+        nc.sync.dma_start(out=beta_all[:], in_=beta.partition_broadcast(P))
 
-        p2 = keep.tile([128, 4, 4, 2], BF16, name="p2")
-        pm2 = keep.tile([128, 2, 4, 2], BF16, name="pm2")
-        pq = keep.tile([128, 2, 2, 2], BF16, name="pq")
-        p1 = keep.tile([128, 6, 2, 2], BF16, name="p1")
-        pb = keep.tile([128, 2, 2], BF16, name="pb")
-        stdf = keep.tile([128, 16], F32, name="stdf")
-        sbias = keep.tile([128, 16], F32, name="sbias")
-        icap = keep.tile([128, 8], F32, name="icap")
-        nab = keep.tile([128, 8, 2], F32, name="nab")
-        icpm = keep.tile([128, 4, 2], F32, name="icpm")
-        pbias = keep.tile([128, 4, 2], F32, name="pbias")
+        def slopes_of(n):
+            return slopes[:, 2 * n : 2 * n + 2, :, :].rearrange("p g t c -> p (g t c)")
 
-        def flat2(n):
-            return p2[:, 2 * n : 2 * n + 2, :, :].rearrange("p g t c -> p (g t c)")
-
-        def flat1(n):
-            return p1[:, 2 * n : 2 * n + 2, :, :].rearrange("p g u e -> p (g u e)")
+        def cells_of(n):
+            return cells[:, 2 * n : 2 * n + 2, :, :].rearrange("p g u e -> p (g u e)")
 
         def sigmoid_parameters():
-            bank = psum.tile([128, 4, 128], F32, name="wT")
+            bank = psum.tile([P, 4, P], F32, name="words")
             for t in range(4):
-                nc.tensor.transpose(bank[:, t, :], pr2[:].bitcast(F32)[:, t::4], ident[:])
-            nc.vector.tensor_copy(out=p2[:].rearrange("p r t c -> p r (t c)").bitcast(F32), in_=bank[:, :, 0:4].rearrange("p t r -> p r t"))
-            nc.vector.tensor_copy(out=stdf[:], in_=flat2(0))
-            nc.vector.scalar_tensor_tensor(out=sbias[:], in0=flat2(1), scalar=-1.0, in1=flat2(0), op0=ALU.mult, op1=ALU.mult)
+                nc.tensor.transpose(bank[:, t, :], slope_rows[:].bitcast(F32)[:, t::4], ident[:])
+            nc.vector.tensor_copy(out=slopes[:].rearrange("p r t c -> p r (t c)").bitcast(F32), in_=bank[:, :, 0:4].rearrange("p t r -> p r t"))
+            nc.vector.tensor_copy(out=std_col[:], in_=slopes_of(0))
+            nc.vector.scalar_tensor_tensor(out=sigmoid_bias[:], in0=slopes_of(1), scalar=-1.0, in1=slopes_of(0), op0=ALU.mult, op1=ALU.mult)
 
         def current_parameters():
-            bank = psum.tile([128, 4, 128], F32, name="hp")
+            bank = psum.tile([P, 4, P], F32, name="h_sums")
             for t in range(4):
-                nc.tensor.transpose(bank[:, t, :], prm[:].bitcast(F32)[:, t::4], ident[:])
-            nc.vector.tensor_copy(out=pm2[:].rearrange("p r t c -> p r (t c)").bitcast(F32), in_=bank[:, :, 0:2].rearrange("p t r -> p r t"))
-            bank = psum.tile([128, 4, 128], F32, name="hp")
+                nc.tensor.transpose(bank[:, t, :], max_rows[:].bitcast(F32)[:, t::4], ident[:])
+            nc.vector.tensor_copy(out=maxima[:].rearrange("p r t c -> p r (t c)").bitcast(F32), in_=bank[:, :, 0:2].rearrange("p t r -> p r t"))
+            bank = psum.tile([P, 4, P], F32, name="h_sums")
             for u in range(2):
-                nc.tensor.transpose(bank[:, u, :], pr1[:].bitcast(F32)[:, u::2], ident[:])
-            nc.vector.tensor_copy(out=p1[:].rearrange("p r u e -> p r (u e)").bitcast(F32), in_=bank[:, 0:2, 0:6].rearrange("p u r -> p r u"))
-            nc.vector.reciprocal(out=icap[:], in_=flat1(0))
+                nc.tensor.transpose(bank[:, u, :], cell_rows[:].bitcast(F32)[:, u::2], ident[:])
+            nc.vector.tensor_copy(out=cells[:].rearrange("p r u e -> p r (u e)").bitcast(F32), in_=bank[:, 0:2, 0:6].rearrange("p u r -> p r u"))
+            nc.vector.reciprocal(out=inv_cap[:], in_=cells_of(0))
             nc.vector.scalar_tensor_tensor(
-                out=nab[:], in0=pm2[:].rearrange("p g t c -> p (g t) c"), scalar=-1.0,
-                in1=icap[:].unsqueeze(2).to_broadcast([128, 8, 2]), op0=ALU.mult, op1=ALU.mult)
+                out=minus_ab[:], in0=maxima[:].rearrange("p g t c -> p (g t) c"), scalar=-1.0,
+                in1=inv_cap[:].unsqueeze(2).to_broadcast([P, SETS, 2]), op0=ALU.mult, op1=ALU.mult)
 
         def bias_parameters():
-            bank = psum.tile([128, 4, 128], F32, name="hp")
+            bank = psum.tile([P, 4, P], F32, name="h_sums")
             for u in range(2):
-                nc.tensor.transpose(bank[:, u, :], prb[:].bitcast(F32)[:, u::2], ident[:])
-            nc.tensor.transpose(bank[:, 2, :], prb[:].bitcast(F32)[:, 0:128], ident[:])
-            nc.vector.tensor_copy(out=pq[:].rearrange("p r u e -> p r (u e)").bitcast(F32), in_=bank[:, 0:2, 0:2].rearrange("p u r -> p r u"))
-            nc.vector.tensor_copy(out=pb[:].rearrange("p g u -> p (g u)").bitcast(F32), in_=bank[:, 2, 2:4])
+                nc.tensor.transpose(bank[:, u, :], bias_rows[:].bitcast(F32)[:, u::2], ident[:])
+            nc.tensor.transpose(bank[:, 2, :], bias_rows[:].bitcast(F32)[:, 0:P], ident[:])
+            nc.scalar.copy(out=b1_col[:].rearrange("p r u e -> p r (u e)").bitcast(F32), in_=bank[:, 0:2, 0:2].rearrange("p u r -> p r u"))
+            nc.scalar.copy(out=b2_col[:].rearrange("p g u -> p (g u)").bitcast(F32), in_=bank[:, 2, 2:4])
 
         def spread_scale():
-            bank = psum.tile([128, 512], F32, name="hp")
-            nc.tensor.matmul(bank[:], lhsT=ident[:, 0:1].to_broadcast([128, 128]), rhs=prf[:], start=True, stop=True)
-            nc.vector.tensor_copy(out=scl[:], in_=bank[:])
+            bank = psum.tile([P, 512], F32, name="h_sums")
+            nc.tensor.matmul(bank[:], lhsT=ident[:, 0:1].to_broadcast([P, P]), rhs=scale_row[:], start=True, stop=True)
+            nc.scalar.copy(out=input_scale[:], in_=bank[:])
 
         def pre_parameters():
-            icv = icap[:].rearrange("p (q e) -> p q e", e=2)
-            nc.vector.tensor_copy(out=icpm[:, :, 0:1], in_=icv[:, :, 0:1])
-            nc.vector.tensor_scalar(out=icpm[:, :, 1:2], in0=icv[:, :, 1:2], scalar1=-1.0, scalar2=None, op0=ALU.mult)
-            nc.vector.tensor_tensor(
-                out=pbias[:], in0=icpm[:], in1=pb[:].rearrange("p g u -> p (g u)").unsqueeze(2).to_broadcast([128, 4, 2]), op=ALU.mult)
-            nc.vector.tensor_tensor(out=pbias[:], in0=pbias[:], in1=p1[:, 2:4, :, :].rearrange("p g u e -> p (g u) e"), op=ALU.add)
+            by_parity = inv_cap[:].rearrange("p (q e) -> p q e", e=2)
+            for e in range(2):
+                nc.gpsimd.tensor_scalar(
+                    out=pre_scale[:, :, e : e + 1], in0=by_parity[:, :, e : e + 1], scalar1=1.0 - 2.0 * e, scalar2=0.0, op0=ALU.mult, op1=ALU.add)
+            nc.gpsimd.tensor_tensor(
+                out=pre_bias[:], in0=pre_scale[:], in1=b2_col[:].rearrange("p g u -> p (g u)").unsqueeze(2).to_broadcast([P, 4, 2]), op=ALU.mult)
+            nc.gpsimd.tensor_tensor(out=pre_bias[:], in0=pre_bias[:], in1=cells_of(1).rearrange("p (q e) -> p q e", e=2), op=ALU.add)
 
-        def exc(idx):
-            return p1[:, 2:4, :, :].rearrange("p g u e -> p (g u e)")[:, idx : idx + 1]
+        def turn_w1(kg):
+            nc.vector.tensor_copy(out=w1_turned[kg][:].rearrange("p (g t m) -> p g m t", g=2, t=4), in_=w1_words[kg][:].rearrange("p (g m t) -> p g m t", g=2, t=4))
 
-        def inh(idx):
-            return p1[:, 4:6, :, :].rearrange("p g u e -> p (g u e)")[:, idx : idx + 1]
+        def turn_w1_scales():
+            nc.vector.tensor_copy(out=w1_scales_turned[:].rearrange("p (g t m) -> p g m t", g=2, t=4), in_=w1_scales[:].rearrange("p (g m t) -> p g m t", g=2, t=4))
 
-        def permute_w1(k):
-            nc.vector.tensor_copy(out=w1p[k][:].rearrange("p (g t m) -> p g m t", g=2, t=4), in_=w1w[k][:].rearrange("p (g m t) -> p g m t", g=2, t=4))
+        def turn_w2():
+            for kg in range(2):
+                nc.vector.tensor_copy(out=w2_turned[:, kg, :].rearrange("p (g u m) -> p g m u", g=2, u=2), in_=w2_words[:, kg, :].rearrange("p (g m u) -> p g m u", g=2, u=2))
+            nc.vector.tensor_copy(out=w2_scales_turned[:].rearrange("p (g u m) -> p g m u", g=2, u=2), in_=w2_scales[:].rearrange("p (g m u) -> p g m u", g=2, u=2))
 
-        def permute_w1_scales():
-            nc.vector.tensor_copy(out=w1sp[:].rearrange("p (g t m) -> p g m t", g=2, t=4), in_=w1s[:].rearrange("p (g m t) -> p g m t", g=2, t=4))
-
-        def permute_w2(k):
-            nc.vector.tensor_copy(out=w2p[:, k, :].rearrange("p (g u m) -> p g m u", g=2, u=2), in_=w2w[:, k, :].rearrange("p (g m u) -> p g m u", g=2, u=2))
-
-        def permute_w2_scales():
-            nc.vector.tensor_copy(out=w2sp[:].rearrange("p (g u m) -> p g m u", g=2, u=2), in_=w2s[:].rearrange("p (g m u) -> p g m u", g=2, u=2))
-
-        groups = ((0,), (1,), (2,), (3,))
-        rows = [256 * len(pairs) for pairs in groups]
-        home = {k: (n, 256 * pairs.index(k)) for n, pairs in enumerate(groups) for k in pairs}
-        vT = {}
-        P0 = {}
-        P1 = {}
-        st = {}
-
-        def cat_words(k, kg):
-            bank = psum.tile([128, 2, 256], F32, name="wT")
-            for j in range(2):
-                src = st[k, "x", j][:] if kg == 0 else sts[k][:, j, :]
-                off = 0 if kg == 0 else 256 * (kg - 1)
-                for u in range(2):
-                    nc.tensor.transpose(bank[:, u, 128 * j : 128 * j + 128], src.bitcast(F32)[:, off + u : off + 256 : 2], ident[:])
-            st[k, "bank", kg] = bank
-
-        def cat_copy(k, kg, on_vector=False):
-            if kg == 0:
-                st[k, "q", 0] = work.tile([128, 256, 4], BF16, name="inT", align_bytes=64)
-            else:
-                n, r0 = home[k]
-                if kg == 1 and r0 == 0:
-                    vT[n] = work.tile([128, 2, rows[n], 4], BF16, name="vT", align_bytes=64, bufs=3)
-                st[k, "q", kg] = vT[n][:, kg - 1, r0 : r0 + 256, :]
-            dst = st[k, "q", kg][:].bitcast(F32) if kg == 0 else st[k, "q", kg].bitcast(F32)
-            src = st[k, "bank", kg][:].rearrange("p u n -> p n u")
-            if on_vector:
-                nc.vector.tensor_copy(out=dst, in_=src)
-            else:
-                nc.scalar.copy(out=dst, in_=src)
-
-        def cat_quantize(k, kg):
-            if (k, "cc") not in st:
-                st[k, "cc"] = work.tile([128, 3, 256], I32, name="cc", align_bytes=64)
-                st[k, "cs"] = work.tile([128, 3, 256], U8, name="cs", align_bytes=64)
-            src = st[k, "q", kg][:] if kg == 0 else st[k, "q", kg]
-            nc.vector.quantize_mx(out=st[k, "cc"][:, kg, :].bitcast(FP8X4), scales=st[k, "cs"][:, kg, :], in_=src.rearrange("p n t -> p (n t)"))
+        made = {}
 
         def widen(k, j):
-            x = work.tile([128, 512], BF16, name="xw", bufs=4)
-            nc.vector.tensor_tensor(out=x[:], in0=xb[k][:, j, :].bitcast(FP8), in1=scl[:], op=ALU.mult)
-            st[k, "x", j] = x
+            x = work.tile([P, 512], BF16, name="inputs", bufs=4)
+            nc.vector.tensor_tensor(out=x[:], in0=input_bytes[k][:, j, :].bitcast(FP8), in1=input_scale[:], op=ALU.mult)
+            made["inputs", k, j] = x
+
+        def cat_words(k, kg):
+            bank = psum.tile([P, 2, PAIR], F32, name="words")
+            for j in range(2):
+                rows = made["inputs", k, j][:] if kg == 0 else state_rows[k][:, j, :]
+                first = 0 if kg == 0 else 256 * (kg - 1)
+                for u in range(2):
+                    nc.tensor.transpose(bank[:, u, P * j : P * j + P], rows.bitcast(F32)[:, first + u : first + 256 : 2], ident[:])
+            made["words", k, kg] = bank
+
+        def cat_copy(k, kg, copy=nc.scalar.copy):
+            if kg == 0:
+                made["inputs_turned", k] = work.tile([P, PAIR, 4], BF16, name="inputs_turned", align_bytes=64)
+                turned = made["inputs_turned", k][:]
+            else:
+                if kg == 1:
+                    made["states", k] = work.tile([P, 2, PAIR, 4], BF16, name="states_turned", align_bytes=64, bufs=3)
+                turned = made["states", k][:, kg - 1, :, :]
+            copy(out=turned.bitcast(F32), in_=made["words", k, kg][:].rearrange("p u n -> p n u"))
+
+        def cat_quantize_states(k):
+            made["cat", k] = work.tile([P, 3, PAIR], I32, name="cat_codes", align_bytes=64)
+            made["cat_scales", k] = work.tile([P, 3, PAIR], U8, name="cat_scales", align_bytes=64)
+            nc.vector.quantize_mx(
+                out=made["cat", k][:, 1:3, :].rearrange("p g n -> p (g n)").bitcast(FP8X4), scales=made["cat_scales", k][:, 1:3, :].rearrange("p g n -> p (g n)"),
+                in_=made["states", k][:].rearrange("p g n t -> p (g n t)"))
+
+        def cat_quantize_inputs(k):
+            nc.vector.quantize_mx(
+                out=made["cat", k][:, 0, :].bitcast(FP8X4), scales=made["cat_scales", k][:, 0, :], in_=made["inputs_turned", k][:].rearrange("p n t -> p (n t)"))
 
         def h_matmul(k, j, g):
-            acc = psum.tile([128, 4, 128], F32, name="hp")
-            rows_j = slice(128 * j, 128 * j + 128)
+            acc = psum.tile([P, 4, P], F32, name="h_sums")
+            rows_j = slice(P * j, P * j + P)
             for t in range(4):
-                cols = slice(512 * g + 128 * t, 512 * g + 128 * t + 128)
+                cols = slice(512 * g + P * t, 512 * g + P * t + P)
                 for kg in (1, 2, 0):
                     nc.tensor.matmul_mx(
                         out=acc[:, t, :],
-                        lhsT=w1p[kg][:, cols].bitcast(FP8X4), lhsT_scale=w1sp[4 * kg : 128, cols],
-                        rhs=st[k, "cc"][:, kg, rows_j].bitcast(FP8X4), rhs_scale=st[k, "cs"][:, kg, rows_j],
+                        lhsT=w1_turned[kg][:, cols].bitcast(FP8X4), lhsT_scale=w1_scales_turned[4 * kg : P, cols],
+                        rhs=made["cat", k][:, kg, rows_j].bitcast(FP8X4), rhs_scale=made["cat_scales", k][:, kg, rows_j],
                         start=(kg == 1), stop=(kg == 0))
-            st[k, "hp", j, g] = acc
+            made["acc", k, j, g] = acc
 
         def h_add(k, j, g):
             if j == 0 and g == 0:
-                st[k, "hT"] = work.tile([128, 2, 256, 4], BF16, name="hT", align_bytes=64)
-            bias = pq[:].rearrange("p g u e -> p (g u e)")[:, 4 * g : 4 * g + 4].unsqueeze(1).to_broadcast([128, 128, 4])
-            nc.vector.tensor_tensor(out=st[k, "hT"][:, g, 128 * j : 128 * j + 128, :], in0=st[k, "hp", j, g][:].rearrange("p t n -> p n t"), in1=bias, op=ALU.add)
+                made["h", k] = work.tile([P, 2, PAIR, 4], BF16, name="h_turned", align_bytes=64)
+            bias = b1_col[:].rearrange("p g u e -> p (g u e)")[:, 4 * g : 4 * g + 4].unsqueeze(1).to_broadcast([P, P, 4])
+            nc.vector.tensor_tensor(
+                out=made["h", k][:, g, P * j : P * j + P, :], in0=made["acc", k, j, g][:].rearrange("p t n -> p n t"), in1=bias, op=ALU.add)
 
-        def h_quantize(k, g):
-            if g == 0:
-                st[k, "hc"] = work.tile([128, 2, 256], I32, name="hc", align_bytes=64)
-                st[k, "hs"] = work.tile([128, 2, 256], U8, name="hs", align_bytes=64)
-            nc.vector.quantize_mx(out=st[k, "hc"][:, g, :].bitcast(FP8X4), scales=st[k, "hs"][:, g, :], in_=st[k, "hT"][:, g, :, :].rearrange("p n t -> p (n t)"))
+        def h_quantize(k):
+            made["h_codes", k] = work.tile([P, 2, PAIR], I32, name="h_codes", align_bytes=64)
+            made["h_scales", k] = work.tile([P, 2, PAIR], U8, name="h_scales", align_bytes=64)
+            nc.vector.quantize_mx(
+                out=made["h_codes", k][:].rearrange("p g n -> p (g n)").bitcast(FP8X4), scales=made["h_scales", k][:].rearrange("p g n -> p (g n)"),
+                in_=made["h", k][:].rearrange("p g n t -> p (g n t)"))
 
         def pre_matmul(k, g):
-            acc = psum.tile([128, 2, 256], F32, name="pp")
+            acc = psum.tile([P, 2, PAIR], F32, name="pre_sums")
             for u in range(2):
-                cols = slice(256 * g + 128 * u, 256 * g + 128 * u + 128)
+                cols = slice(256 * g + P * u, 256 * g + P * u + P)
                 for kg in range(2):
                     nc.tensor.matmul_mx(
                         out=acc[:, u, :],
-                        lhsT=w2p[:, kg, cols].bitcast(FP8X4), lhsT_scale=w2sp[4 * kg : 128, cols],
-                        rhs=st[k, "hc"][:, kg, :].bitcast(FP8X4), rhs_scale=st[k, "hs"][:, kg, :],
+                        lhsT=w2_turned[:, kg, cols].bitcast(FP8X4), lhsT_scale=w2_scales_turned[4 * kg : P, cols],
+                        rhs=made["h_codes", k][:, kg, :].bitcast(FP8X4), rhs_scale=made["h_scales", k][:, kg, :],
                         start=(kg == 0), stop=(kg == 1))
-            st[k, "pp", g] = acc
+            made["pre", k, g] = acc
 
         def pre_copy(k, idx):
             if idx == 0:
-                st[k, "pm"] = work.tile([128, 8, 256], F32, name="pm", bufs=3)
+                made["input_term", k] = work.tile([P, SETS, PAIR], F32, name="input_term", bufs=3)
             nc.scalar.activation(
-                out=st[k, "pm"][:, idx, :], in_=st[k, "pp", idx // 4][:, (idx % 4) // 2, :], func=ACT.Identity,
-                scale=icpm[:].rearrange("p q e -> p (q e)")[:, idx : idx + 1], bias=pbias[:].rearrange("p q e -> p (q e)")[:, idx : idx + 1])
+                out=made["input_term", k][:, idx, :], in_=made["pre", k, idx // 4][:, (idx % 4) // 2, :], func=ACT.Identity,
+                scale=pre_scale[:].rearrange("p q e -> p (q e)")[:, idx : idx + 1], bias=pre_bias[:].rearrange("p q e -> p (q e)")[:, idx : idx + 1])
 
         def sigmoids(k, idx):
             g, t = idx // 4, idx % 4
-            s0 = work.tile([128, rows[k]], F32, name="s0", bufs=4)
-            s1 = work.tile([128, rows[k]], F32, name="s1", bufs=4)
-            nc.scalar.activation(out=s0[:], in_=vT[k][:, g, :, t], func=ACT.Sigmoid, scale=stdf[:, 2 * idx : 2 * idx + 1], bias=sbias[:, 2 * idx : 2 * idx + 1])
-            nc.scalar.activation(out=s1[:], in_=vT[k][:, g, :, t ^ 1], func=ACT.Sigmoid, scale=stdf[:, 2 * idx + 1 : 2 * idx + 2], bias=sbias[:, 2 * idx + 1 : 2 * idx + 2])
-            st[k, "s", idx] = (s0, s1)
+            s0 = work.tile([P, PAIR], F32, name="s0", bufs=4)
+            s1 = work.tile([P, PAIR], F32, name="s1", bufs=4)
+            for s, c, source in ((s0, 0, t), (s1, 1, t ^ 1)):
+                col = 2 * idx + c
+                nc.scalar.activation(
+                    out=s[:], in_=made["states", k][:, g, :, source], func=ACT.Sigmoid, scale=std_col[:, col : col + 1], bias=sigmoid_bias[:, col : col + 1])
+            made["s", k, idx] = (s0, s1)
 
-        def conductances(k, idx):
-            s0, s1 = st[k, "s", idx]
-            nabf = nab[:].rearrange("p i c -> p (i c)")
-            nc.scalar.activation(out=s0[:], in_=s0[:], func=ACT.Identity, scale=nabf[:, 2 * idx : 2 * idx + 1], bias=1.0)
-            nc.scalar.activation(out=s1[:], in_=s1[:], func=ACT.Copy, scale=nabf[:, 2 * idx + 1 : 2 * idx + 2])
+        def factors(k, idx):
+            s0, s1 = made["s", k, idx]
+            nc.scalar.activation(out=s0[:], in_=s0[:], func=ACT.Identity, scale=minus_ab[:, idx, 0:1], bias=1.0)
+            nc.scalar.activation(out=s1[:], in_=s1[:], func=ACT.Copy, scale=minus_ab[:, idx, 1:2])
 
         def currents(k, idx):
             g, t = idx // 4, idx % 4
             if idx == 0:
-                P0[k] = work.tile([128, 8, rows[k]], F32, name="P0", bufs=3)
-                P1[k] = work.tile([128, 8, rows[k]], F32, name="P1", bufs=3)
-            s0, s1 = st[k, "s", idx]
-            own = vT[k][:, g, :, t]
-            nc.vector.scalar_tensor_tensor(out=P0[k][:, idx, :], in0=own, scalar=exc(idx), in1=s0[:], op0=ALU.subtract, op1=ALU.mult)
-            nc.vector.scalar_tensor_tensor(out=P1[k][:, idx, :], in0=own, scalar=inh(idx), in1=s1[:], op0=ALU.subtract, op1=ALU.mult)
+                made["exc_term", k] = work.tile([P, SETS, PAIR], F32, name="exc_term", bufs=3)
+                made["inh_term", k] = work.tile([P, SETS, PAIR], F32, name="inh_term", bufs=3)
+            own = made["states", k][:, g, :, t]
+            for name, n, s in (("exc_term", 1, made["s", k, idx][0]), ("inh_term", 2, made["s", k, idx][1])):
+                nc.vector.scalar_tensor_tensor(
+                    out=made[name, k][:, idx, :], in0=own, scalar=cells_of(n)[:, idx : idx + 1], in1=s[:], op0=ALU.subtract, op1=ALU.mult)
 
         def sum_terms(i, g):
             k, j = i // 2, i % 2
-            n, r0 = home[k]
-            tok = slice(128 * j, 128 * j + 128)
-            gtok = slice(r0 + 128 * j, r0 + 128 * j + 128)
-            x = psum.tile([128, 512], F32, name=("xp", "xp", "xp", "xp", "xp", "hp", "xp", "pp")[i], bufs=2)
+            rows_j = slice(P * j, P * j + P)
+            x = psum.tile([P, 512], F32, name=X_BANKS[i], bufs=2)
             for t in range(4):
                 idx = 4 * g + t
-                terms = (P0[n][:, idx, gtok], P1[n][:, idx, gtok], st[k, "pm"][:, idx, tok])
-                for m in range(3):
-                    nc.tensor.matmul(x[:, 128 * t : 128 * t + 128], lhsT=terms[m], rhs=ident[:], is_transpose=True, start=(m == 0), stop=(m == 2))
-            st[i, "xp", g] = x
+                for n, name in enumerate(("exc_term", "inh_term", "input_term")):
+                    nc.tensor.matmul(
+                        x[:, P * t : P * t + P], lhsT=made[name, k][:, idx, rows_j], rhs=ident[:], is_transpose=True, start=(n == 0), stop=(n == 2))
+            made["x", i, g] = x
 
-        def row_stats(i, g):
+        def reciprocal_deviation(i, square, factor):
+            variance = work.tile([P, 1], F32, name="variance", bufs=4)
+            rstd = work.tile([P, 1], F32, name="rstd", bufs=4)
+            nc.gpsimd.tensor_scalar(out=variance[:], in0=square, scalar1=factor, scalar2=EPS, op0=ALU.mult, op1=ALU.add)
+            nc.gpsimd.tensor_tensor(out=rstd[:], in0=variance[:], in1=minus_half[:], op=ALU.pow)
+            made["rstd", i] = rstd
+
+        def vector_stats(i, g):
             if g == 0:
-                st[i, "stats"] = work.tile([128, 2, 6], F32, name="stats")
-            nc.vector.bn_stats(out=st[i, "stats"][:, g, :], in_=st[i, "xp", g][:])
+                made["stats", i] = work.tile([P, 2, 6], F32, name="stats", bufs=4)
+            nc.vector.bn_stats(out=made["stats", i][:, g, :], in_=made["x", i, g][:])
 
-        def row_aggregate(i):
-            mv = work.tile([128, 2], F32, name="mv")
-            nc.vector.bn_aggr(out=mv[:], in_=st[i, "stats"][:].rearrange("p g s -> p (g s)"))
-            st[i, "mu"] = mv[:, 0:1]
-            row_rstd(i, mv[:, 1:2], 1.0)
+        def vector_aggregate(i):
+            mean_var = work.tile([P, 2], F32, name="mean_var", bufs=4)
+            nc.vector.bn_aggr(out=mean_var[:], in_=made["stats", i][:].rearrange("p g s -> p (g s)"))
+            made["mean", i] = mean_var[:, 0:1]
+            reciprocal_deviation(i, mean_var[:, 1:2], 1.0)
 
-        def row_rstd(i, square, factor):
-            ve = work.tile([128, 1], F32, name="ve")
-            rstd = work.tile([128, 1], F32, name="rstd")
-            nc.gpsimd.tensor_scalar(out=ve[:], in0=square, scalar1=factor, scalar2=1e-6, op0=ALU.mult, op1=ALU.add)
-            nc.gpsimd.tensor_tensor(out=rstd[:], in0=ve[:], in1=mhalf[:], op=ALU.pow)
-            st[i, "rstd"] = rstd
-
-        def row_sum(i, g):
+        def scalar_sum(i, g):
             if g == 0:
-                st[i, "sums"] = work.tile([128, 4], F32, name="sums")
-            junk = work.tile([128, 512], F32, name="junk")
-            nc.scalar.activation(out=junk[:], in_=st[i, "xp", g][:], func=ACT.Copy, accum_out=st[i, "sums"][:, g : g + 1])
+                made["sums", i] = work.tile([P, 4], F32, name="sums", bufs=4)
+            scratch = work.tile([P, 512], F32, name="scratch")
+            nc.scalar.activation(out=scratch[:], in_=made["x", i, g][:], func=ACT.Copy, accum_out=made["sums", i][:, g : g + 1])
 
-        def row_mean(i):
-            mean = work.tile([128, 2], F32, name="mean")
-            total = work.tile([128, 1], F32, name="total")
-            nc.gpsimd.tensor_tensor(out=total[:], in0=st[i, "sums"][:, 0:1], in1=st[i, "sums"][:, 1:2], op=ALU.add)
-            nc.gpsimd.tensor_scalar(out=mean[:, 0:1], in0=total[:], scalar1=-1.0 / 1024.0, scalar2=0.0, op0=ALU.mult, op1=ALU.add)
-            nc.gpsimd.tensor_scalar(out=mean[:, 1:2], in0=total[:], scalar1=1.0 / 1024.0, scalar2=0.0, op0=ALU.mult, op1=ALU.add)
-            st[i, "mu"], st[i, "negmu"] = mean[:, 1:2], mean[:, 0:1]
+        def scalar_mean(i):
+            mean = work.tile([P, 2], F32, name="mean", bufs=4)
+            total = work.tile([P, 1], F32, name="total", bufs=4)
+            nc.gpsimd.tensor_tensor(out=total[:], in0=made["sums", i][:, 0:1], in1=made["sums", i][:, 1:2], op=ALU.add)
+            for n, sign in enumerate((-1.0, 1.0)):
+                nc.gpsimd.tensor_scalar(out=mean[:, n : n + 1], in0=total[:], scalar1=sign / 1024.0, scalar2=0.0, op0=ALU.mult, op1=ALU.add)
+            made["minus_mean", i], made["mean", i] = mean[:, 0:1], mean[:, 1:2]
 
-        def row_square(i, g):
-            junk = work.tile([128, 512], F32, name="junk")
-            nc.scalar.activation(out=junk[:], in_=st[i, "xp", g][:], func=ACT.Square, bias=st[i, "negmu"], accum_out=st[i, "sums"][:, 2 + g : 3 + g])
+        def scalar_square(i, g):
+            scratch = work.tile([P, 512], F32, name="scratch")
+            nc.scalar.activation(
+                out=scratch[:], in_=made["x", i, g][:], func=ACT.Square, bias=made["minus_mean", i], accum_out=made["sums", i][:, 2 + g : 3 + g])
 
-        def row_variance(i):
-            total = work.tile([128, 1], F32, name="total")
-            nc.gpsimd.tensor_tensor(out=total[:], in0=st[i, "sums"][:, 2:3], in1=st[i, "sums"][:, 3:4], op=ALU.add)
-            row_rstd(i, total[:], 1.0 / 1024.0)
+        def scalar_variance(i):
+            total = work.tile([P, 1], F32, name="total", bufs=4)
+            nc.gpsimd.tensor_tensor(out=total[:], in0=made["sums", i][:, 2:3], in1=made["sums", i][:, 3:4], op=ALU.add)
+            reciprocal_deviation(i, total[:], 1.0 / 1024.0)
 
-        def row_center(i, g):
+        def center(i, g):
             if g == 0:
-                st[i, "y"] = work.tile([128, 1024], F32, name="y")
+                made["y", i] = work.tile([P, 1024], F32, name="y", bufs=3)
             cols = slice(512 * g, 512 * g + 512)
             nc.vector.scalar_tensor_tensor(
-                out=st[i, "y"][:, cols].rearrange("p (q t) -> p q t", t=4), in0=st[i, "xp", g][:].rearrange("p (t q) -> p q t", t=4),
-                scalar=st[i, "mu"], in1=gmc[:, cols].rearrange("p (q t) -> p q t", t=4), op0=ALU.subtract, op1=ALU.mult)
+                out=made["y", i][:, cols].rearrange("p (q t) -> p q t", t=4), in0=made["x", i, g][:].rearrange("p (t q) -> p q t", t=4),
+                scalar=made["mean", i], in1=gamma_all[:, cols].rearrange("p (q t) -> p q t", t=4), op0=ALU.subtract, op1=ALU.mult)
 
-        def row_store(i, g):
-            if g == 0:
-                st[i, "o"] = work.tile([128, 1024], F32, name="o")
-            cols = slice(512 * g, 512 * g + 512) if i in (7,) else slice(0, 1024)
-            o = st[i, "o"]
-            if i not in (7,) and g == 0:
-                return
-            nc.vector.scalar_tensor_tensor(out=o[:, cols], in0=st[i, "y"][:, cols], scalar=st[i, "rstd"][:, 0:1], in1=btc[:, cols], op0=ALU.mult, op1=ALU.add)
-            nc.sync.dma_start(out=out[128 * i : 128 * i + 128, cols], in_=o[:, cols])
+        def finish(i):
+            o = work.tile([P, 1024], F32, name="o")
+            parts = 2 if i == 7 else 1
+            for n in range(parts):
+                cols = slice(1024 // parts * n, 1024 // parts * (n + 1))
+                nc.vector.scalar_tensor_tensor(
+                    out=o[:, cols], in0=made["y", i][:, cols], scalar=made["rstd", i][:, 0:1], in1=beta_all[:, cols], op0=ALU.mult, op1=ALU.add)
+                nc.sync.dma_start(out=out[P * i : P * i + P, cols], in_=o[:, cols])
 
         plan = {}
 
         def place(kind, slot, *calls):
             plan.setdefault((slot, kind), []).extend(calls)
 
-        def place_norm(i, s, d):
+        def place_norm(i):
+            s = NORM_START[i]
             place("norm", s, (sum_terms, i, 0))
-            if i in (5, 7):
-                place("norm", s + d[0], (sum_terms, i, 1), (row_sum, i, 0))
-                place("norm", s + d[1], (row_sum, i, 1), (row_mean, i))
-                place("norm", s + d[2], (row_square, i, 0), (row_square, i, 1), (row_variance, i))
+            if i in SCALAR_STATS:
+                d = SCALAR_NORM_STEPS
+                place("norm", s + d[0], (sum_terms, i, 1), (scalar_sum, i, 0))
+                place("norm", s + d[1], (scalar_sum, i, 1), (scalar_mean, i))
+                place("norm", s + d[2], (scalar_square, i, 0), (scalar_square, i, 1), (scalar_variance, i))
             else:
-                place("norm", s + d[0], (sum_terms, i, 1), (row_stats, i, 0))
-                place("norm", s + d[1], (row_stats, i, 1))
-                place("norm", s + d[2], (row_aggregate, i))
-            place("norm", s + d[3], (row_center, i, 0), (row_center, i, 1))
-            place("norm", s + d[4], (row_store, i, 0), (row_store, i, 1))
+                d = LAST_NORM_STEPS if i == 6 else NORM_STEPS
+                place("norm", s + d[0], (sum_terms, i, 1), (vector_stats, i, 0))
+                place("norm", s + d[1], (vector_stats, i, 1))
+                place("norm", s + d[2], (vector_aggregate, i))
+            place("norm", s + d[3], (center, i, 0), (center, i, 1))
+            place("norm", s + d[4], (finish, i))
 
-        def place_chain(k, s, d):
-            place("chain", s, (cat_words, k, 1), (widen, k, 0))
-            place("chain", s + d[0], (cat_copy, k, 1), (cat_words, k, 2), (widen, k, 1))
-            place("chain", s + d[1], (cat_copy, k, 2), (cat_words, k, 0), (cat_quantize, k, 1))
-            place("chain", s + d[2], (cat_copy, k, 0), (cat_quantize, k, 2))
-            place("chain", s + d[3], (cat_quantize, k, 0))
+        def place_cat(k):
+            s, d = CAT_START[k - 1], CAT_STEPS
+            place("pair", s, (cat_words, k, 1), (widen, k, 0))
+            place("pair", s + d[0], (cat_copy, k, 1), (cat_words, k, 2), (widen, k, 1))
+            place("pair", s + d[1], (cat_copy, k, 2), (cat_words, k, 0))
+            place("pair", s + d[2], (cat_copy, k, 0), (cat_quantize_states, k))
+            place("pair", s + d[3], (cat_quantize_inputs, k))
 
-        def place_rest(k, s, e):
-            order = ((0, 0), (1, 0), (0, 1), (1, 1))
-            for n in range(4):
-                j, g = order[n]
-                place("chain", s + e[2 * n], (h_matmul, k, j, g))
-                place("chain", s + e[2 * n + 1], (h_add, k, j, g))
-                if j == 1:
-                    place("chain", s + e[8 + g], (h_quantize, k, g))
-            place("chain", s + e[10], (pre_matmul, k, 0))
-            place("chain", s + e[11], (pre_copy, k, 0), (pre_copy, k, 1))
-            place("chain", s + e[12], (pre_matmul, k, 1), (pre_copy, k, 2), (pre_copy, k, 3))
-            place("chain", s + e[13], (pre_copy, k, 4), (pre_copy, k, 5))
-            place("chain", s + e[14], (pre_copy, k, 6), (pre_copy, k, 7))
+        def place_products(k):
+            s, d = PRODUCT_START[k], PRODUCT_STEPS
+            for n, (j, g) in enumerate(((0, 0), (1, 0), (0, 1), (1, 1))):
+                place("pair", s + d[2 * n], (h_matmul, k, j, g))
+                place("pair", s + d[2 * n + 1], (h_add, k, j, g))
+            place("pair", s + d[8], (h_quantize, k))
+            place("pair", s + d[9], (pre_matmul, k, 0))
+            place("pair", s + d[10], (pre_copy, k, 0), (pre_copy, k, 1))
+            place("pair", s + d[11], (pre_matmul, k, 1), (pre_copy, k, 2), (pre_copy, k, 3))
+            place("pair", s + d[12], (pre_copy, k, 4), (pre_copy, k, 5))
+            place("pair", s + d[13], (pre_copy, k, 6), (pre_copy, k, 7))
 
-        chain_at = (4, 8, 15)
-        rest_at = (6, 11, 17, 20)
-        norm_at = (16, 19, 22, 25, 29, 31, 36, 40)
         for i in range(8):
-            place_norm(i, norm_at[i], (2, 2, 3, 3, 7) if i in (5, 7) else (1, 1, 2, 3, 4) if i < 6 else (1, 4, 4, 4, 4))
-        for k in range(4):
-            for idx in range(8):
-                place("sigmoid", 8 * k + idx, (sigmoids, k, idx))
-                place("current", 8 * k + idx + 3, (currents, k, idx))
-                place("conduct", 8 * k + idx, (conductances, k, idx))
+            place_norm(i)
+        for k in range(PAIRS):
+            for idx in range(SETS):
+                place("sigmoid", SETS * k + idx, (sigmoids, k, idx))
+                place("current", SETS * k + idx + CURRENT_STEP, (currents, k, idx))
+                place("factor", SETS * k + idx, (factors, k, idx))
             if k > 0:
-                place_chain(k, chain_at[k - 1], (1, 2, 4, 5))
-            place_rest(k, rest_at[k], (0, 1, 1, 2, 2, 3, 3, 4, 3, 5, 6, 7, 8, 9, 8))
-        place("chain", (3, 1, 2, 5, 5)[0], (cat_quantize, 0, 1), (permute_w1, 2))
-        place("chain", (3, 1, 2, 5, 5)[1], (cat_quantize, 0, 2), (cat_words, 0, 0), (permute_w1, 0))
-        place("chain", (3, 1, 2, 5, 5)[2], (cat_copy, 0, 0), (bias_parameters,), (pre_parameters,), (permute_w1_scales,))
-        place("chain", (3, 1, 2, 5, 5)[3], (cat_quantize, 0, 0))
-        place("chain", (3, 1, 2, 5, 5)[4], (permute_w2, 0), (permute_w2, 1), (permute_w2_scales,))
+                place_cat(k)
+            place_products(k)
+
+        head = (
+            (cat_quantize_states, 0), (cat_words, 0, 0), (turn_w1, 0), (cat_copy, 0, 0), (bias_parameters,), (pre_parameters,), (turn_w1_scales,),
+            (turn_w1, 2), (cat_quantize_inputs, 0), (turn_w2,))
+        for slot, call in zip(HEAD, head):
+            place("pair", slot, call)
         cat_words(0, 1)
-        cat_copy(0, 1, True)
+        cat_copy(0, 1, nc.vector.tensor_copy)
         sigmoid_parameters()
         current_parameters()
         cat_words(0, 2)
-        cat_copy(0, 2, True)
+        cat_copy(0, 2, nc.vector.tensor_copy)
         spread_scale()
         widen(0, 0)
         widen(0, 1)
-        permute_w1(1)
-        for slot in range(0, max(key[0] for key in plan) + 1):
-            lists = [plan.get((slot, kind), []) for kind in ("norm", "current", "chain")]
+        turn_w1(1)
+
+        for slot in range(max(key[0] for key in plan) + 1):
             for call in plan.get((slot, "sigmoid"), []):
                 call[0](*call[1:])
+            lists = [plan.get((slot, kind), []) for kind in ("norm", "current", "pair")]
             for n in range(max(len(calls) for calls in lists)):
                 for calls in lists:
                     if n < len(calls):
                         calls[n][0](*calls[n][1:])
-            for call in plan.get((slot, "conduct"), []):
+            for call in plan.get((slot, "factor"), []):
                 call[0](*call[1:])

from contextlib import ExitStack

import concourse.mybir as mybir
from concourse.masks import make_identity

F32 = mybir.dt.float32
BF16 = mybir.dt.bfloat16
I32 = mybir.dt.int32
U8 = mybir.dt.uint8
FP8 = mybir.dt.float8_e4m3fn
FP8X4 = mybir.dt.float8_e4m3fn_x4
ALU = mybir.AluOpType
ACT = mybir.ActivationFunctionType

FLOPS = 2 * 1024 * (1536 * 1024 + 1024 * 512)

P = 128
SETS = 8
PAIRS = 4
PAIR = 2 * P
EPS = 1e-6

CAT_START = (4, 8, 12)
CAT_STEPS = (2, 3, 4, 6)
PRODUCT_START = (6, 11, 16, 20)
PRODUCT_STEPS = (0, 1, 1, 2, 2, 3, 3, 4, 5, 6, 7, 8, 9, 9)
CURRENT_STEP = 2
NORM_START = (15, 18, 22, 24, 27, 29, 33, 36)
NORM_STEPS = (1, 2, 2, 3, 4)
LAST_NORM_STEPS = (0, 1, 3, 3, 8)
SCALAR_NORM_STEPS = (1, 2, 3, 5, 7)
HEAD = (1, 1, 2, 3, 2, 4, 1, 3, 4, 7)

SCALAR_STATS = (3, 5, 7)
X_BANKS = ("x", "x", "x", "words", "x", "words", "h_sums", "pre_sums")


def tile_memorylayercell_pa_w8_kernel(
    tc, inputs_bytes, inputs_scale, states, W1_words, W1_scales, b1, W2_words, W2_scales, b2,
    excitatory_potential, inhibitory_potential, capacitance, max_conductance,
    mean_conductance_potential, std_conductance, gamma, beta, out):
    nc = tc.nc
    with ExitStack() as ctx:
        keep = ctx.enter_context(tc.tile_pool(name="keep", bufs=1))
        work = ctx.enter_context(tc.tile_pool(name="work", bufs=2))
        psum = ctx.enter_context(tc.psum_pool(name="psum", bufs=2))
        ctx.enter_context(tc.manual_schedule())

        slope_rows = keep.tile([P, 1024], BF16, name="slope_rows")
        max_rows = keep.tile([P, 1024], BF16, name="max_rows")
        cell_rows = keep.tile([P, 512], BF16, name="cell_rows")
        bias_rows = keep.tile([P, 512], BF16, name="bias_rows")
        scale_row = keep.tile([P, 512], F32, name="scale_row")
        state_rows = [keep.tile([P, 2, 1024], BF16, name="state_rows%d" % k) for k in range(PAIRS)]
        input_bytes = [keep.tile([P, 2, 512], U8, name="input_bytes%d" % k) for k in range(PAIRS)]
        input_scale = keep.tile([P, 512], F32, name="input_scale")
        w1_words = [keep.tile([P, 1024], I32, name="w1_words%d" % kg, align_bytes=64) for kg in range(3)]
        w1_scales = keep.tile([P, 1024], U8, name="w1_scales", align_bytes=64)
        w2_words = keep.tile([P, 2, 512], I32, name="w2_words", align_bytes=64)
        w2_turned = keep.tile([P, 2, 512], I32, name="w2_turned", align_bytes=64)
        w2_scales = keep.tile([P, 512], U8, name="w2_scales", align_bytes=64)
        w2_scales_turned = keep.tile([P, 512], U8, name="w2_scales_turned", align_bytes=64)
        w1_turned = [keep.tile([P, 1024], I32, name="w1_turned%d" % kg, align_bytes=64) for kg in range(3)]
        w1_scales_turned = keep.tile([P, 1024], U8, name="w1_scales_turned", align_bytes=64)
        gamma_all = keep.tile([P, 1024], BF16, name="gamma_all")
        beta_all = keep.tile([P, 1024], BF16, name="beta_all")
        ident = keep.tile([P, P], F32, name="ident")
        minus_half = keep.tile([P, 1], F32, name="minus_half")
        warm = keep.tile([P, 1], F32, name="warm")

        slopes = keep.tile([P, 4, 4, 2], BF16, name="slopes")
        maxima = keep.tile([P, 2, 4, 2], BF16, name="maxima")
        b1_col = keep.tile([P, 2, 2, 2], BF16, name="b1_col")
        cells = keep.tile([P, 6, 2, 2], BF16, name="cells")
        b2_col = keep.tile([P, 2, 2], BF16, name="b2_col")
        std_col = keep.tile([P, 16], F32, name="std_col")
        sigmoid_bias = keep.tile([P, 16], F32, name="sigmoid_bias")
        inv_cap = keep.tile([P, SETS], F32, name="inv_cap")
        minus_ab = keep.tile([P, SETS, 2], F32, name="minus_ab")
        pre_scale = keep.tile([P, 4, 2], F32, name="pre_scale")
        pre_bias = keep.tile([P, 4, 2], F32, name="pre_bias")

        def load_states(k):
            nc.sync.dma_start(out=state_rows[k][:], in_=states[PAIR * k : PAIR * k + PAIR, :].rearrange("(i p) s -> p i s", p=P))

        def load_bytes(k):
            nc.sync.dma_start(out=input_bytes[k][:], in_=inputs_bytes[PAIR * k : PAIR * k + PAIR, :].rearrange("(i p) k -> p i k", p=P))

        def load_conductance(dst, n, src):
            nc.sync.dma_start(out=dst[2 * n : 2 * n + 2, :], in_=src.rearrange("(g x) c -> g (x c)", g=2))

        def load_vector(dst, n, src, queue):
            queue.dma_start(out=dst[2 * n : 2 * n + 2, :], in_=src.rearrange("(g x) -> g x", g=2))

        nc.vector.memset(warm[:], 0.0)
        nc.scalar.activation(out=warm[:], in_=warm[:], func=ACT.Sigmoid)

        nc.vector.memset(slope_rows[:].bitcast(I32), 0)
        nc.vector.memset(scale_row[:], 0.0)
        nc.vector.memset(max_rows[:].bitcast(I32), 0)
        nc.vector.memset(cell_rows[:].bitcast(I32), 0)
        nc.vector.memset(w1_scales[:].bitcast(I32), 0)
        nc.vector.memset(w2_scales[:].bitcast(I32), 0)
        make_identity(nc, ident[:])
        nc.gpsimd.memset(minus_half[:], -0.5)
        nc.gpsimd.memset(bias_rows[:].bitcast(I32), 0)

        nc.sync.dma_start(out=state_rows[0][:, 0, :], in_=states[0:P, :])
        load_conductance(slope_rows, 0, std_conductance)
        load_conductance(slope_rows, 1, mean_conductance_potential)
        nc.sync.dma_start(out=state_rows[0][:, 1, :], in_=states[P:PAIR, :])
        load_conductance(max_rows, 0, max_conductance)
        load_vector(cell_rows, 0, capacitance, nc.sync)
        load_vector(cell_rows, 1, excitatory_potential, nc.sync)
        load_vector(cell_rows, 2, inhibitory_potential, nc.sync)
        nc.sync.dma_start(out=scale_row[0:1, :], in_=inputs_scale)
        load_bytes(0)
        for kg in (1, 2, 0):
            nc.sync.dma_start(out=w1_words[kg][:], in_=W1_words[kg].rearrange("p n t -> p (n t)").bitcast(I32))
        for q in range(4):
            nc.sync.dma_start(out=w1_scales[32 * q : 32 * q + 12, :].bitcast(I32), in_=W1_scales[:, 4 * q : 4 * q + 4, :].bitcast(I32))
        load_vector(bias_rows, 0, b1, nc.gpsimd)
        nc.gpsimd.dma_start(out=bias_rows[2:4, 0:256], in_=b2.rearrange("(g x) -> g x", g=2))
        load_states(1)
        load_bytes(1)
        nc.sync.dma_start(out=w2_words[:], in_=W2_words.rearrange("k p n t -> p k (n t)").bitcast(I32))
        for q in range(4):
            nc.sync.dma_start(out=w2_scales[32 * q : 32 * q + 8, :].bitcast(I32), in_=W2_scales[:, 4 * q : 4 * q + 4, :].bitcast(I32))
        for k in range(2, PAIRS):
            load_states(k)
            load_bytes(k)
        nc.sync.dma_start(out=gamma_all[:], in_=gamma.partition_broadcast(P))
        nc.sync.dma_start(out=beta_all[:], in_=beta.partition_broadcast(P))

        def slopes_of(n):
            return slopes[:, 2 * n : 2 * n + 2, :, :].rearrange("p g t c -> p (g t c)")

        def cells_of(n):
            return cells[:, 2 * n : 2 * n + 2, :, :].rearrange("p g u e -> p (g u e)")

        def sigmoid_parameters():
            bank = psum.tile([P, 4, P], F32, name="words")
            for t in range(4):
                nc.tensor.transpose(bank[:, t, :], slope_rows[:].bitcast(F32)[:, t::4], ident[:])
            nc.vector.tensor_copy(out=slopes[:].rearrange("p r t c -> p r (t c)").bitcast(F32), in_=bank[:, :, 0:4].rearrange("p t r -> p r t"))
            nc.vector.tensor_copy(out=std_col[:], in_=slopes_of(0))
            nc.vector.scalar_tensor_tensor(out=sigmoid_bias[:], in0=slopes_of(1), scalar=-1.0, in1=slopes_of(0), op0=ALU.mult, op1=ALU.mult)

        def current_parameters():
            bank = psum.tile([P, 4, P], F32, name="h_sums")
            for t in range(4):
                nc.tensor.transpose(bank[:, t, :], max_rows[:].bitcast(F32)[:, t::4], ident[:])
            nc.vector.tensor_copy(out=maxima[:].rearrange("p r t c -> p r (t c)").bitcast(F32), in_=bank[:, :, 0:2].rearrange("p t r -> p r t"))
            bank = psum.tile([P, 4, P], F32, name="h_sums")
            for u in range(2):
                nc.tensor.transpose(bank[:, u, :], cell_rows[:].bitcast(F32)[:, u::2], ident[:])
            nc.vector.tensor_copy(out=cells[:].rearrange("p r u e -> p r (u e)").bitcast(F32), in_=bank[:, 0:2, 0:6].rearrange("p u r -> p r u"))
            nc.vector.reciprocal(out=inv_cap[:], in_=cells_of(0))
            nc.vector.scalar_tensor_tensor(
                out=minus_ab[:], in0=maxima[:].rearrange("p g t c -> p (g t) c"), scalar=-1.0,
                in1=inv_cap[:].unsqueeze(2).to_broadcast([P, SETS, 2]), op0=ALU.mult, op1=ALU.mult)

        def bias_parameters():
            bank = psum.tile([P, 4, P], F32, name="h_sums")
            for u in range(2):
                nc.tensor.transpose(bank[:, u, :], bias_rows[:].bitcast(F32)[:, u::2], ident[:])
            nc.tensor.transpose(bank[:, 2, :], bias_rows[:].bitcast(F32)[:, 0:P], ident[:])
            nc.scalar.copy(out=b1_col[:].rearrange("p r u e -> p r (u e)").bitcast(F32), in_=bank[:, 0:2, 0:2].rearrange("p u r -> p r u"))
            nc.scalar.copy(out=b2_col[:].rearrange("p g u -> p (g u)").bitcast(F32), in_=bank[:, 2, 2:4])

        def spread_scale():
            bank = psum.tile([P, 512], F32, name="h_sums")
            nc.tensor.matmul(bank[:], lhsT=ident[:, 0:1].to_broadcast([P, P]), rhs=scale_row[:], start=True, stop=True)
            nc.scalar.copy(out=input_scale[:], in_=bank[:])

        def pre_parameters():
            by_parity = inv_cap[:].rearrange("p (q e) -> p q e", e=2)
            for e in range(2):
                nc.gpsimd.tensor_scalar(
                    out=pre_scale[:, :, e : e + 1], in0=by_parity[:, :, e : e + 1], scalar1=1.0 - 2.0 * e, scalar2=0.0, op0=ALU.mult, op1=ALU.add)
            nc.gpsimd.tensor_tensor(
                out=pre_bias[:], in0=pre_scale[:], in1=b2_col[:].rearrange("p g u -> p (g u)").unsqueeze(2).to_broadcast([P, 4, 2]), op=ALU.mult)
            nc.gpsimd.tensor_tensor(out=pre_bias[:], in0=pre_bias[:], in1=cells_of(1).rearrange("p (q e) -> p q e", e=2), op=ALU.add)

        def turn_w1(kg):
            nc.vector.tensor_copy(out=w1_turned[kg][:].rearrange("p (g t m) -> p g m t", g=2, t=4), in_=w1_words[kg][:].rearrange("p (g m t) -> p g m t", g=2, t=4))

        def turn_w1_scales():
            nc.vector.tensor_copy(out=w1_scales_turned[:].rearrange("p (g t m) -> p g m t", g=2, t=4), in_=w1_scales[:].rearrange("p (g m t) -> p g m t", g=2, t=4))

        def turn_w2():
            for kg in range(2):
                nc.vector.tensor_copy(out=w2_turned[:, kg, :].rearrange("p (g u m) -> p g m u", g=2, u=2), in_=w2_words[:, kg, :].rearrange("p (g m u) -> p g m u", g=2, u=2))
            nc.vector.tensor_copy(out=w2_scales_turned[:].rearrange("p (g u m) -> p g m u", g=2, u=2), in_=w2_scales[:].rearrange("p (g m u) -> p g m u", g=2, u=2))

        made = {}

        def widen(k, j):
            x = work.tile([P, 512], BF16, name="inputs", bufs=4)
            nc.vector.tensor_tensor(out=x[:], in0=input_bytes[k][:, j, :].bitcast(FP8), in1=input_scale[:], op=ALU.mult)
            made["inputs", k, j] = x

        def cat_words(k, kg):
            bank = psum.tile([P, 2, PAIR], F32, name="words")
            for j in range(2):
                rows = made["inputs", k, j][:] if kg == 0 else state_rows[k][:, j, :]
                first = 0 if kg == 0 else 256 * (kg - 1)
                for u in range(2):
                    nc.tensor.transpose(bank[:, u, P * j : P * j + P], rows.bitcast(F32)[:, first + u : first + 256 : 2], ident[:])
            made["words", k, kg] = bank

        def cat_copy(k, kg, copy=nc.scalar.copy):
            if kg == 0:
                made["inputs_turned", k] = work.tile([P, PAIR, 4], BF16, name="inputs_turned", align_bytes=64)
                turned = made["inputs_turned", k][:]
            else:
                if kg == 1:
                    made["states", k] = work.tile([P, 2, PAIR, 4], BF16, name="states_turned", align_bytes=64, bufs=3)
                turned = made["states", k][:, kg - 1, :, :]
            copy(out=turned.bitcast(F32), in_=made["words", k, kg][:].rearrange("p u n -> p n u"))

        def cat_quantize_states(k):
            made["cat", k] = work.tile([P, 3, PAIR], I32, name="cat_codes", align_bytes=64)
            made["cat_scales", k] = work.tile([P, 3, PAIR], U8, name="cat_scales", align_bytes=64)
            nc.vector.quantize_mx(
                out=made["cat", k][:, 1:3, :].rearrange("p g n -> p (g n)").bitcast(FP8X4), scales=made["cat_scales", k][:, 1:3, :].rearrange("p g n -> p (g n)"),
                in_=made["states", k][:].rearrange("p g n t -> p (g n t)"))

        def cat_quantize_inputs(k):
            nc.vector.quantize_mx(
                out=made["cat", k][:, 0, :].bitcast(FP8X4), scales=made["cat_scales", k][:, 0, :], in_=made["inputs_turned", k][:].rearrange("p n t -> p (n t)"))

        def h_matmul(k, j, g):
            acc = psum.tile([P, 4, P], F32, name="h_sums")
            rows_j = slice(P * j, P * j + P)
            for t in range(4):
                cols = slice(512 * g + P * t, 512 * g + P * t + P)
                for kg in (1, 2, 0):
                    nc.tensor.matmul_mx(
                        out=acc[:, t, :],
                        lhsT=w1_turned[kg][:, cols].bitcast(FP8X4), lhsT_scale=w1_scales_turned[4 * kg : P, cols],
                        rhs=made["cat", k][:, kg, rows_j].bitcast(FP8X4), rhs_scale=made["cat_scales", k][:, kg, rows_j],
                        start=(kg == 1), stop=(kg == 0))
            made["acc", k, j, g] = acc

        def h_add(k, j, g):
            if j == 0 and g == 0:
                made["h", k] = work.tile([P, 2, PAIR, 4], BF16, name="h_turned", align_bytes=64)
            bias = b1_col[:].rearrange("p g u e -> p (g u e)")[:, 4 * g : 4 * g + 4].unsqueeze(1).to_broadcast([P, P, 4])
            nc.vector.tensor_tensor(
                out=made["h", k][:, g, P * j : P * j + P, :], in0=made["acc", k, j, g][:].rearrange("p t n -> p n t"), in1=bias, op=ALU.add)

        def h_quantize(k):
            made["h_codes", k] = work.tile([P, 2, PAIR], I32, name="h_codes", align_bytes=64)
            made["h_scales", k] = work.tile([P, 2, PAIR], U8, name="h_scales", align_bytes=64)
            nc.vector.quantize_mx(
                out=made["h_codes", k][:].rearrange("p g n -> p (g n)").bitcast(FP8X4), scales=made["h_scales", k][:].rearrange("p g n -> p (g n)"),
                in_=made["h", k][:].rearrange("p g n t -> p (g n t)"))

        def pre_matmul(k, g):
            acc = psum.tile([P, 2, PAIR], F32, name="pre_sums")
            for u in range(2):
                cols = slice(256 * g + P * u, 256 * g + P * u + P)
                for kg in range(2):
                    nc.tensor.matmul_mx(
                        out=acc[:, u, :],
                        lhsT=w2_turned[:, kg, cols].bitcast(FP8X4), lhsT_scale=w2_scales_turned[4 * kg : P, cols],
                        rhs=made["h_codes", k][:, kg, :].bitcast(FP8X4), rhs_scale=made["h_scales", k][:, kg, :],
                        start=(kg == 0), stop=(kg == 1))
            made["pre", k, g] = acc

        def pre_copy(k, idx):
            if idx == 0:
                made["input_term", k] = work.tile([P, SETS, PAIR], F32, name="input_term", bufs=3)
            nc.scalar.activation(
                out=made["input_term", k][:, idx, :], in_=made["pre", k, idx // 4][:, (idx % 4) // 2, :], func=ACT.Identity,
                scale=pre_scale[:].rearrange("p q e -> p (q e)")[:, idx : idx + 1], bias=pre_bias[:].rearrange("p q e -> p (q e)")[:, idx : idx + 1])

        def sigmoids(k, idx):
            g, t = idx // 4, idx % 4
            s0 = work.tile([P, PAIR], F32, name="s0", bufs=4)
            s1 = work.tile([P, PAIR], F32, name="s1", bufs=4)
            for s, c, source in ((s0, 0, t), (s1, 1, t ^ 1)):
                col = 2 * idx + c
                nc.scalar.activation(
                    out=s[:], in_=made["states", k][:, g, :, source], func=ACT.Sigmoid, scale=std_col[:, col : col + 1], bias=sigmoid_bias[:, col : col + 1])
            made["s", k, idx] = (s0, s1)

        def factors(k, idx):
            s0, s1 = made["s", k, idx]
            nc.scalar.activation(out=s0[:], in_=s0[:], func=ACT.Identity, scale=minus_ab[:, idx, 0:1], bias=1.0)
            nc.scalar.activation(out=s1[:], in_=s1[:], func=ACT.Copy, scale=minus_ab[:, idx, 1:2])

        def currents(k, idx):
            g, t = idx // 4, idx % 4
            if idx == 0:
                made["exc_term", k] = work.tile([P, SETS, PAIR], F32, name="exc_term", bufs=3)
                made["inh_term", k] = work.tile([P, SETS, PAIR], F32, name="inh_term", bufs=3)
            own = made["states", k][:, g, :, t]
            for name, n, s in (("exc_term", 1, made["s", k, idx][0]), ("inh_term", 2, made["s", k, idx][1])):
                nc.vector.scalar_tensor_tensor(
                    out=made[name, k][:, idx, :], in0=own, scalar=cells_of(n)[:, idx : idx + 1], in1=s[:], op0=ALU.subtract, op1=ALU.mult)

        def sum_terms(i, g):
            k, j = i // 2, i % 2
            rows_j = slice(P * j, P * j + P)
            x = psum.tile([P, 512], F32, name=X_BANKS[i], bufs=2)
            for t in range(4):
                idx = 4 * g + t
                for n, name in enumerate(("exc_term", "inh_term", "input_term")):
                    nc.tensor.matmul(
                        x[:, P * t : P * t + P], lhsT=made[name, k][:, idx, rows_j], rhs=ident[:], is_transpose=True, start=(n == 0), stop=(n == 2))
            made["x", i, g] = x

        def reciprocal_deviation(i, square, factor):
            variance = work.tile([P, 1], F32, name="variance", bufs=4)
            rstd = work.tile([P, 1], F32, name="rstd", bufs=4)
            nc.gpsimd.tensor_scalar(out=variance[:], in0=square, scalar1=factor, scalar2=EPS, op0=ALU.mult, op1=ALU.add)
            nc.gpsimd.tensor_tensor(out=rstd[:], in0=variance[:], in1=minus_half[:], op=ALU.pow)
            made["rstd", i] = rstd

        def vector_stats(i, g):
            if g == 0:
                made["stats", i] = work.tile([P, 2, 6], F32, name="stats", bufs=4)
            nc.vector.bn_stats(out=made["stats", i][:, g, :], in_=made["x", i, g][:])

        def vector_aggregate(i):
            mean_var = work.tile([P, 2], F32, name="mean_var", bufs=4)
            nc.vector.bn_aggr(out=mean_var[:], in_=made["stats", i][:].rearrange("p g s -> p (g s)"))
            made["mean", i] = mean_var[:, 0:1]
            reciprocal_deviation(i, mean_var[:, 1:2], 1.0)

        def scalar_sum(i, g):
            if g == 0:
                made["sums", i] = work.tile([P, 4], F32, name="sums", bufs=4)
            scratch = work.tile([P, 512], F32, name="scratch")
            nc.scalar.activation(out=scratch[:], in_=made["x", i, g][:], func=ACT.Copy, accum_out=made["sums", i][:, g : g + 1])

        def scalar_mean(i):
            mean = work.tile([P, 2], F32, name="mean", bufs=4)
            total = work.tile([P, 1], F32, name="total", bufs=4)
            nc.gpsimd.tensor_tensor(out=total[:], in0=made["sums", i][:, 0:1], in1=made["sums", i][:, 1:2], op=ALU.add)
            for n, sign in enumerate((-1.0, 1.0)):
                nc.gpsimd.tensor_scalar(out=mean[:, n : n + 1], in0=total[:], scalar1=sign / 1024.0, scalar2=0.0, op0=ALU.mult, op1=ALU.add)
            made["minus_mean", i], made["mean", i] = mean[:, 0:1], mean[:, 1:2]

        def scalar_square(i, g):
            scratch = work.tile([P, 512], F32, name="scratch")
            nc.scalar.activation(
                out=scratch[:], in_=made["x", i, g][:], func=ACT.Square, bias=made["minus_mean", i], accum_out=made["sums", i][:, 2 + g : 3 + g])

        def scalar_variance(i):
            total = work.tile([P, 1], F32, name="total", bufs=4)
            nc.gpsimd.tensor_tensor(out=total[:], in0=made["sums", i][:, 2:3], in1=made["sums", i][:, 3:4], op=ALU.add)
            reciprocal_deviation(i, total[:], 1.0 / 1024.0)

        def center(i, g):
            if g == 0:
                made["y", i] = work.tile([P, 1024], F32, name="y", bufs=3)
            cols = slice(512 * g, 512 * g + 512)
            nc.vector.scalar_tensor_tensor(
                out=made["y", i][:, cols].rearrange("p (q t) -> p q t", t=4), in0=made["x", i, g][:].rearrange("p (t q) -> p q t", t=4),
                scalar=made["mean", i], in1=gamma_all[:, cols].rearrange("p (q t) -> p q t", t=4), op0=ALU.subtract, op1=ALU.mult)

        def finish(i):
            o = work.tile([P, 1024], F32, name="o")
            parts = 2 if i == 7 else 1
            for n in range(parts):
                cols = slice(1024 // parts * n, 1024 // parts * (n + 1))
                nc.vector.scalar_tensor_tensor(
                    out=o[:, cols], in0=made["y", i][:, cols], scalar=made["rstd", i][:, 0:1], in1=beta_all[:, cols], op0=ALU.mult, op1=ALU.add)
                nc.sync.dma_start(out=out[P * i : P * i + P, cols], in_=o[:, cols])

        plan = {}

        def place(kind, slot, *calls):
            plan.setdefault((slot, kind), []).extend(calls)

        def place_norm(i):
            s = NORM_START[i]
            place("norm", s, (sum_terms, i, 0))
            if i in SCALAR_STATS:
                d = SCALAR_NORM_STEPS
                place("norm", s + d[0], (sum_terms, i, 1), (scalar_sum, i, 0))
                place("norm", s + d[1], (scalar_sum, i, 1), (scalar_mean, i))
                place("norm", s + d[2], (scalar_square, i, 0), (scalar_square, i, 1), (scalar_variance, i))
            else:
                d = LAST_NORM_STEPS if i == 6 else NORM_STEPS
                place("norm", s + d[0], (sum_terms, i, 1), (vector_stats, i, 0))
                place("norm", s + d[1], (vector_stats, i, 1))
                place("norm", s + d[2], (vector_aggregate, i))
            place("norm", s + d[3], (center, i, 0), (center, i, 1))
            place("norm", s + d[4], (finish, i))

        def place_cat(k):
            s, d = CAT_START[k - 1], CAT_STEPS
            place("pair", s, (cat_words, k, 1), (widen, k, 0))
            place("pair", s + d[0], (cat_copy, k, 1), (cat_words, k, 2), (widen, k, 1))
            place("pair", s + d[1], (cat_copy, k, 2), (cat_words, k, 0))
            place("pair", s + d[2], (cat_copy, k, 0), (cat_quantize_states, k))
            place("pair", s + d[3], (cat_quantize_inputs, k))

        def place_products(k):
            s, d = PRODUCT_START[k], PRODUCT_STEPS
            for n, (j, g) in enumerate(((0, 0), (1, 0), (0, 1), (1, 1))):
                place("pair", s + d[2 * n], (h_matmul, k, j, g))
                place("pair", s + d[2 * n + 1], (h_add, k, j, g))
            place("pair", s + d[8], (h_quantize, k))
            place("pair", s + d[9], (pre_matmul, k, 0))
            place("pair", s + d[10], (pre_copy, k, 0), (pre_copy, k, 1))
            place("pair", s + d[11], (pre_matmul, k, 1), (pre_copy, k, 2), (pre_copy, k, 3))
            place("pair", s + d[12], (pre_copy, k, 4), (pre_copy, k, 5))
            place("pair", s + d[13], (pre_copy, k, 6), (pre_copy, k, 7))

        for i in range(8):
            place_norm(i)
        for k in range(PAIRS):
            for idx in range(SETS):
                place("sigmoid", SETS * k + idx, (sigmoids, k, idx))
                place("current", SETS * k + idx + CURRENT_STEP, (currents, k, idx))
                place("factor", SETS * k + idx, (factors, k, idx))
            if k > 0:
                place_cat(k)
            place_products(k)

        head = (
            (cat_quantize_states, 0), (cat_words, 0, 0), (turn_w1, 0), (cat_copy, 0, 0), (bias_parameters,), (pre_parameters,), (turn_w1_scales,),
            (turn_w1, 2), (cat_quantize_inputs, 0), (turn_w2,))
        for slot, call in zip(HEAD, head):
            place("pair", slot, call)
        cat_words(0, 1)
        cat_copy(0, 1, nc.vector.tensor_copy)
        sigmoid_parameters()
        current_parameters()
        cat_words(0, 2)
        cat_copy(0, 2, nc.vector.tensor_copy)
        spread_scale()
        widen(0, 0)
        widen(0, 1)
        turn_w1(1)

        for slot in range(max(key[0] for key in plan) + 1):
            for call in plan.get((slot, "sigmoid"), []):
                call[0](*call[1:])
            lists = [plan.get((slot, kind), []) for kind in ("norm", "current", "pair")]
            for n in range(max(len(calls) for calls in lists)):
                for calls in lists:
                    if n < len(calls):
                        calls[n][0](*calls[n][1:])
            for call in plan.get((slot, "factor"), []):
                call[0](*call[1:])
